import numpy as np
import ml_dtypes


def mxq(x, axis, fmt="e4m3"):
    dtype, down = {"e4m3": (ml_dtypes.float8_e4m3fn, 7), "e5m2": (ml_dtypes.float8_e5m2, 14)}[fmt]
    v = np.moveaxis(np.asarray(x, np.float32).astype(ml_dtypes.bfloat16).astype(np.float64), axis, -1)
    blocks = v.reshape(v.shape[:-1] + (-1, 32))
    amax = np.abs(blocks).max(-1, keepdims=True)
    byte = np.maximum(np.where(amax > 0, np.frexp(amax)[1] - 1 + 127, 0) - down, 1)
    scale = np.exp2(byte - 127.0)
    codes = (blocks / scale).astype(np.float32).astype(dtype).astype(np.float64)
    return np.moveaxis((codes * scale).reshape(v.shape), -1, axis)


WIDE = False


def mx_kscale(k):
    if not WIDE:
        return np.ones(k)
    levels = np.array([10, -10, 5, -5, 0])
    if k % 512:
        return np.exp2(np.random.permutation(np.resize(levels, k // 32))).repeat(32)
    a = np.empty((k // 512, 16))
    for p in range(k // 512):
        a[p, :8] = np.random.permutation(np.resize(levels, 8))
        for g in range(8):
            far = levels[np.abs(levels - a[p, g]) >= 10]
            a[p, g + 8] = far[np.random.randint(len(far))]
    return np.exp2(a.ravel()).repeat(32)


BF16 = ml_dtypes.bfloat16


def bf(x):
    return np.asarray(x, np.float32).astype(BF16)


def f64(x):
    return np.asarray(x).astype(np.float64)


B, T, N, H, G, GH = 32, 4, 8, 512, 9, 3


def sigmoid(v):
    return 1.0 / (1.0 + np.exp(-v))


def draw0():
    s = mx_kscale(H)
    return {"h_new": bf(np.random.standard_normal((B, T, N, H)) * 0.35 * s),
            "c_new": bf(np.random.standard_normal((B, T, N, H)) * 0.8),
            "g_t": bf(np.random.standard_normal((B, N, H)) * s),
            "c_g_t": bf(np.random.standard_normal((B, N, H)) * 0.5),
            "Wg_t": bf(np.random.standard_normal((GH, T, H, H)) * 2.0 / np.sqrt(H) / s[:, None]),
            "Zg_t": bf(np.random.standard_normal((GH, T, H, H)) * 1.0 / np.sqrt(H) / s[:, None]),
            "bg_t": bf(np.random.standard_normal((GH, T, 1, H)) * 0.3)}


def core(h_new, c_new, g_t, c_g_t, Wg_t, Zg_t, bg_t):
    c_new, c_g_t = f64(c_new), f64(c_g_t)
    hq = mxq(f64(h_new).transpose(1, 0, 2, 3).reshape(T, B * N, H), 2, "e4m3")
    preg = (hq @ mxq(f64(Wg_t), 2, "e4m3")) + f64(bg_t)
    zt_part = mxq(f64(g_t).reshape(B * N, H), 1, "e4m3") @ mxq(f64(Zg_t), 2, "e4m3")
    gates = sigmoid(preg + zt_part).reshape(GH, T, B, N, H).transpose(0, 2, 1, 3, 4)
    f_t, gg_t, o_t = gates
    c_g_t_new = np.mean(f_t * c_new, axis=1) + np.mean(gg_t, axis=1) * c_g_t
    g_t_new = np.mean(o_t, axis=1) * np.tanh(c_g_t_new)
    return g_t_new, c_g_t_new


def e4m3fn_bytes(y):
    return np.clip(np.asarray(y, np.float64), -448.0, 448.0).astype(np.float32).astype(ml_dtypes.float8_e4m3fn).view(np.uint8)


def e4m3fn_values(b):
    return np.asarray(b, np.uint8).view(ml_dtypes.float8_e4m3fn).astype(np.float64)


def setup_inputs():
    d = draw0()
    x0 = np.asarray(d['Zg_t']).astype(np.float64)
    s = (np.max(np.abs(x0), axis=(0, 1, 3), keepdims=True) / 448.0).astype(np.float32)
    out = {}
    for k, v in d.items():
        if k == 'Zg_t':
            out['Zg_t_bytes'] = e4m3fn_bytes(x0 / s.astype(np.float64))
            out['Zg_t_scale'] = s
        else:
            out[k] = v
    return out


def reference(h_new, c_new, g_t, c_g_t, Wg_t, Zg_t_bytes, Zg_t_scale, bg_t):
    return core(h_new, c_new, g_t, c_g_t, Wg_t, e4m3fn_values(Zg_t_bytes) * Zg_t_scale.astype(np.float64), bg_t)

@@ -1,0 +1,285 @@
+from contextlib import ExitStack
+
+import concourse.masks as masks
+import concourse.mybir as mybir
+
+FLOPS = 2 * 2 * 12 * 256 * 512 * 512
+
+F32 = mybir.dt.float32
+BF16 = mybir.dt.bfloat16
+U32 = mybir.dt.uint32
+U8 = mybir.dt.uint8
+FP8 = mybir.dt.float8_e4m3fn
+FP8X4 = mybir.dt.float8_e4m3fn_x4
+ACT = mybir.ActivationFunctionType
+ALU = mybir.AluOpType
+
+P = 128
+H = 512
+T = 4
+ROWS = 256
+NFT = 4
+CS = 96
+GATE_ORDER = (1, 0, 2)
+
+
+def tile_st_hmr_pb_kernel(tc, h_new, c_new, g_t, c_g_t, Wg_t, Zg_t_bytes, Zg_t_scale, bg_t, out_0, out_1):
+    nc = tc.nc
+    units = [(g, t) for g in GATE_ORDER for t in range(T)]
+    n_units = len(units)
+
+    h_rows = h_new.rearrange("r t n h -> (r t n) h").rearrange("(i p) h -> p i h", p=P)
+    c_rows = c_new.rearrange("r t n h -> (r t n) h").rearrange("(i p) h -> p i h", p=P)
+    g_rows = g_t.rearrange("r n h -> (r n) h").rearrange("(i p) h -> p i h", p=P)
+    cg_rows = c_g_t.rearrange("r n h -> (r n) h").rearrange("(i p) h -> p i h", p=P)
+    out0_rows = out_0.rearrange("r n h -> (r n) h").rearrange("(i p) h -> p i h", p=P)
+    out1_rows = out_1.rearrange("r n h -> (r n) h").rearrange("(i p) h -> p i h", p=P)
+
+    with ExitStack() as ctx:
+        const = ctx.enter_context(tc.tile_pool(name="const", bufs=1))
+        wpool = ctx.enter_context(tc.tile_pool(name="wpool", bufs=8))
+        zpool = ctx.enter_context(tc.tile_pool(name="zpool", bufs=8))
+        zwpool = ctx.enter_context(tc.tile_pool(name="zwpool", bufs=3))
+        gpool = ctx.enter_context(tc.tile_pool(name="gpool", bufs=3))
+        qpool = ctx.enter_context(tc.tile_pool(name="qpool", bufs=4))
+        spool = ctx.enter_context(tc.tile_pool(name="spool", bufs=2))
+        psum_mm = ctx.enter_context(tc.psum_pool(name="psum_mm", bufs=4))
+        psum_tr = ctx.enter_context(tc.psum_pool(name="psum_tr", bufs=2))
+        psum_acc = ctx.enter_context(tc.psum_pool(name="psum_acc", bufs=2))
+
+        warm_in = const.tile([P, 1], F32, name="warm_in")
+        warm_out = const.tile([P, 1], F32, name="warm_out")
+        nc.vector.memset(warm_in[:], 0.0)
+        nc.scalar.activation(out=warm_out[:], in_=warm_in[:], func=ACT.Sigmoid)
+
+        ident_f = const.tile([P, P], F32, name="ident_f")
+        masks.make_identity(nc, ident_f[:])
+        ident_b = const.tile([P, P], BF16, name="ident_b")
+        masks.make_identity(nc, ident_b[:])
+        perm_f = const.tile([P, P], F32, name="perm_f")
+        nc.vector.tensor_copy(
+            out=perm_f[:].rearrange("p (t r n) -> p t r n", t=4, r=4),
+            in_=ident_f[:].rearrange("p (r t n) -> p t r n", r=4, t=4),
+        )
+        perm_b = const.tile([P, P], BF16, name="perm_b")
+        nc.vector.tensor_copy(
+            out=perm_b[:].rearrange("p (t r n) -> p t r n", t=4, r=4),
+            in_=ident_b[:].rearrange("p (r t n) -> p t r n", r=4, t=4),
+        )
+        bias_raw = const.tile([P, P], BF16, name="bias_raw")
+        nc.vector.memset(bias_raw[:], 0.0)
+
+        zs = const.tile([P, 4], F32, name="zs")
+        nc.sync.dma_start(out=zs[:], in_=Zg_t_scale.rearrange("a b (p j) c -> p (a b j c)", j=4))
+
+        wraw = {}
+        zraw = {}
+
+        def load_unit(u):
+            g, t = units[u]
+            zraw[u] = zpool.tile([P, 4, H], U8, name="zraw", tag="zraw")
+            nc.sync.dma_start(out=zraw[u][:], in_=Zg_t_bytes[g, t].rearrange("(p j) n -> p j n", j=4))
+            wraw[u] = wpool.tile([P, 4, H], BF16, name="wraw", tag="wraw")
+            nc.sync.dma_start(out=wraw[u][:], in_=Wg_t[g, t].rearrange("(p j) n -> p j n", j=4))
+
+        load_unit(0)
+        h_sb = []
+        for q in range(4):
+            hq = const.tile([P, 2, H], BF16, name="h_sb%d" % q)
+            nc.sync.dma_start(out=hq[:], in_=h_rows[:, 2 * q : 2 * q + 2, :])
+            h_sb.append(hq)
+        g_sb = const.tile([P, 2, H], BF16, name="g_sb")
+        nc.sync.dma_start(out=g_sb[:], in_=g_rows)
+        nc.sync.dma_start(out=bias_raw[0:48, :], in_=bg_t.rearrange("g t o (c f) -> (g t o c) f", f=P))
+        for u in range(1, 4):
+            load_unit(u)
+        cg_sb = const.tile([P, 2, H], BF16, name="cg_sb")
+        nc.sync.dma_start(out=cg_sb[:], in_=cg_rows)
+        load_unit(4)
+        c_sb = const.tile([P, 8, H], BF16, name="c_sb")
+        nc.sync.dma_start(out=c_sb[:, 0:4, :], in_=c_rows[:, 0:4, :])
+        nc.sync.dma_start(out=c_sb[:, 4:8, :], in_=c_rows[:, 4:8, :])
+        for u in range(5, n_units):
+            load_unit(u)
+
+        zwide = {}
+        grouped = {}
+        codes = {}
+        scales = {}
+
+        def widen(u):
+            zwide[u] = zwpool.tile([P, 4, H], BF16, name="zwide", tag="zwide")
+            for j in range(4):
+                nc.scalar.activation(
+                    out=zwide[u][:, j, :],
+                    in_=zraw[u][:, j, :].bitcast(FP8),
+                    func=ACT.Copy,
+                    scale=zs[:, j : j + 1],
+                )
+
+        def interleave_w(u):
+            grouped[u] = gpool.tile([P, 2, H, 4], BF16, name="grouped", tag="grouped", align_bytes=64)
+            nc.vector.tensor_copy(out=grouped[u][:, 0, :, :], in_=wraw[u][:].rearrange("p j n -> p n j"))
+
+        def interleave_z(u):
+            nc.scalar.copy(out=grouped[u][:, 1, 0:CS, :], in_=zwide[u][:, :, 0:CS].rearrange("p j n -> p n j"))
+            nc.vector.tensor_copy(out=grouped[u][:, 1, CS:H, :], in_=zwide[u][:, :, CS:H].rearrange("p j n -> p n j"))
+
+        def quantize(u):
+            codes[u] = qpool.tile([P, 2 * H], U32, name="codes", tag="codes", align_bytes=64)
+            scales[u] = qpool.tile([P, 2 * H], U8, name="scales", tag="scales", align_bytes=64)
+            nc.vector.quantize_mx(
+                out=codes[u][:].bitcast(FP8X4),
+                scales=scales[u][:],
+                in_=grouped[u][:].rearrange("p a n j -> p (a n j)"),
+            )
+
+        widen(0)
+        interleave_w(0)
+        interleave_z(0)
+        widen(1)
+
+        hg = const.tile([P, T, ROWS, 4], BF16, name="hg", align_bytes=64)
+        hg32 = hg[:].rearrange("p t r e -> p (t r e)").bitcast(F32).rearrange("p (t r u) -> p t r u", t=T, u=2)
+        for q in range(4):
+            xt = psum_mm.tile([P, 2, 2, P], F32, name="xt", tag="mm")
+            for i2 in range(2):
+                words = h_sb[q][:, i2, :].bitcast(F32)
+                for u2 in range(2):
+                    nc.tensor.transpose(out=xt[:, i2, u2, :], in_=words[:, u2::2], identity=perm_f[:])
+            for i2 in range(2):
+                i = 2 * q + i2
+                nc.scalar.copy(
+                    out=hg32[:, :, 32 * i : 32 * i + 32, :],
+                    in_=xt[:, i2, :, :].rearrange("p u (t r) -> p t r u", t=T),
+                )
+        gg = const.tile([P, ROWS, 4], BF16, name="gg", align_bytes=64)
+        gg32 = gg[:].rearrange("p r e -> p (r e)").bitcast(F32).rearrange("p (i r u) -> p i r u", i=2, u=2)
+        xg = psum_mm.tile([P, 2, 2, P], F32, name="xg", tag="mm")
+        for i2 in range(2):
+            words = g_sb[:, i2, :].bitcast(F32)
+            for u2 in range(2):
+                nc.tensor.transpose(out=xg[:, i2, u2, :], in_=words[:, u2::2], identity=ident_f[:])
+        nc.scalar.copy(out=gg32, in_=xg[:].rearrange("p i u r -> p i r u"))
+
+        bT = psum_tr.tile([P, P], BF16, name="bT", tag="tr")
+        nc.tensor.transpose(out=bT[:], in_=bias_raw[:], identity=ident_b[:])
+        bias_sb = const.tile([P, 48], F32, name="bias_sb")
+        nc.vector.tensor_copy(out=bias_sb[:], in_=bT[:, 0:48])
+
+        h_codes = const.tile([P, T * ROWS], U32, name="h_codes", align_bytes=64)
+        h_scales = const.tile([P, T * ROWS], U8, name="h_scales", align_bytes=64)
+        g_codes = const.tile([P, ROWS], U32, name="g_codes", align_bytes=64)
+        g_scales = const.tile([P, ROWS], U8, name="g_scales", align_bytes=64)
+
+        tmp = const.tile([P, 2, H], F32, name="tmp")
+        cout = const.tile([P, 2, H], F32, name="cout")
+        th = const.tile([P, 2, H], F32, name="th")
+        gout = const.tile([P, 2, H], F32, name="gout")
+
+        sig = {}
+
+        def multiply(u):
+            g, t = units[u]
+            banks = []
+            for b in range(2):
+                mm = psum_mm.tile([P, 2, ROWS], F32, name="mm", tag="mm")
+                for f2 in range(2):
+                    ft = 2 * b + f2
+                    w_cols = slice(ft * P, (ft + 1) * P)
+                    z_cols = slice(H + ft * P, H + (ft + 1) * P)
+                    nc.tensor.matmul_mx(
+                        out=mm[:, f2, :],
+                        lhsT=codes[u][:, w_cols].bitcast(FP8X4),
+                        lhsT_scale=scales[u][:, w_cols],
+                        rhs=h_codes[:, t * ROWS : (t + 1) * ROWS].bitcast(FP8X4),
+                        rhs_scale=h_scales[:, t * ROWS : (t + 1) * ROWS],
+                        start=True,
+                        stop=False,
+                    )
+                    nc.tensor.matmul_mx(
+                        out=mm[:, f2, :],
+                        lhsT=codes[u][:, z_cols].bitcast(FP8X4),
+                        lhsT_scale=scales[u][:, z_cols],
+                        rhs=g_codes[:].bitcast(FP8X4),
+                        rhs_scale=g_scales[:],
+                        start=False,
+                        stop=True,
+                    )
+                banks.append(mm)
+            if t == 0:
+                sig[g] = spool.tile([P, NFT, T, ROWS], F32, name="sig", tag="sig")
+            for b in range(2):
+                for f2 in range(2):
+                    ft = 2 * b + f2
+                    col = (g * T + t) * NFT + ft
+                    nc.scalar.activation(
+                        out=sig[g][:, ft, t, :],
+                        in_=banks[b][:, f2, :],
+                        func=ACT.Sigmoid,
+                        bias=bias_sb[:, col : col + 1],
+                    )
+
+        def sum_frames(g):
+            accs = []
+            for rt in range(2):
+                acc = psum_acc.tile([P, H], F32, name="acc", tag="acc")
+                for ft in range(NFT):
+                    for t in range(T):
+                        nc.tensor.matmul(
+                            out=acc[:, ft * P : (ft + 1) * P],
+                            lhsT=sig[g][:, ft, t, rt * P : (rt + 1) * P],
+                            rhs=ident_f[:],
+                            is_transpose=True,
+                            start=(t == 0),
+                            stop=(t == T - 1),
+                        )
+                accs.append(acc)
+            return accs
+
+        def gate_end(g):
+            if g == 0:
+                for ft in range(NFT):
+                    cT = psum_tr.tile([P, 8, P], BF16, name="cT", tag="tr")
+                    for i in range(8):
+                        nc.tensor.transpose(out=cT[:, i, :], in_=c_sb[:, i, ft * P : (ft + 1) * P], identity=perm_b[:])
+                    view = sig[g][:, ft, :, :].rearrange("p t (i r) -> p t i r", i=8)
+                    nc.vector.tensor_tensor(
+                        out=view, in0=view, in1=cT[:].rearrange("p i (t r) -> p t i r", t=T), op=ALU.mult
+                    )
+            accs = sum_frames(g)
+            for rt in range(2):
+                if g == 1:
+                    nc.vector.scalar_tensor_tensor(
+                        out=tmp[:, rt, :], in0=accs[rt][:], scalar=0.25, in1=cg_sb[:, rt, :], op0=ALU.mult, op1=ALU.mult
+                    )
+                elif g == 0:
+                    nc.vector.scalar_tensor_tensor(
+                        out=cout[:, rt, :], in0=accs[rt][:], scalar=0.25, in1=tmp[:, rt, :], op0=ALU.mult, op1=ALU.add
+                    )
+                    nc.sync.dma_start(out=out1_rows[:, rt, :], in_=cout[:, rt, :])
+                    nc.scalar.activation(out=th[:, rt, :], in_=cout[:, rt, :], func=ACT.Tanh)
+                else:
+                    nc.vector.scalar_tensor_tensor(
+                        out=gout[:, rt, :], in0=accs[rt][:], scalar=0.25, in1=th[:, rt, :], op0=ALU.mult, op1=ALU.mult
+                    )
+                    nc.sync.dma_start(out=out0_rows[:, rt, :], in_=gout[:, rt, :])
+
+        for u in range(n_units):
+            if u + 2 < n_units:
+                widen(u + 2)
+            if u + 1 < n_units:
+                interleave_w(u + 1)
+            quantize(u)
+            if u == 0:
+                nc.vector.quantize_mx(
+                    out=h_codes[:].bitcast(FP8X4), scales=h_scales[:], in_=hg[:].rearrange("p t r e -> p (t r e)")
+                )
+                nc.vector.quantize_mx(
+                    out=g_codes[:].bitcast(FP8X4), scales=g_scales[:], in_=gg[:].rearrange("p r e -> p (r e)")
+                )
+            if u + 1 < n_units:
+                interleave_z(u + 1)
+            multiply(u)
+            if units[u][1] == T - 1:
+                gate_end(units[u][0])

@@ -19,14 +19,14 @@ H = 512
 T = 4
 ROWS = 256
 NFT = 4
-CS = 96
-GATE_ORDER = (1, 0, 2)
+CZ = 96
 
 
 def tile_st_hmr_pb_kernel(tc, h_new, c_new, g_t, c_g_t, Wg_t, Zg_t_bytes, Zg_t_scale, bg_t, out_0, out_1):
     nc = tc.nc
-    units = [(g, t) for g in GATE_ORDER for t in range(T)]
+    units = [(g, t) for g in range(3) for t in range(T)]
     n_units = len(units)
+    last = n_units - 1
 
     h_rows = h_new.rearrange("r t n h -> (r t n) h").rearrange("(i p) h -> p i h", p=P)
     c_rows = c_new.rearrange("r t n h -> (r t n) h").rearrange("(i p) h -> p i h", p=P)
@@ -46,11 +46,14 @@ def tile_st_hmr_pb_kernel(tc, h_new, c_new, g_t, c_g_t, Wg_t, Zg_t_bytes, Zg_t_s
         psum_mm = ctx.enter_context(tc.psum_pool(name="psum_mm", bufs=4))
         psum_tr = ctx.enter_context(tc.psum_pool(name="psum_tr", bufs=2))
         psum_acc = ctx.enter_context(tc.psum_pool(name="psum_acc", bufs=2))
+        ctx.enter_context(tc.manual_schedule())
 
         warm_in = const.tile([P, 1], F32, name="warm_in")
         warm_out = const.tile([P, 1], F32, name="warm_out")
         nc.vector.memset(warm_in[:], 0.0)
         nc.scalar.activation(out=warm_out[:], in_=warm_in[:], func=ACT.Sigmoid)
+        bias_raw = const.tile([P, P], BF16, name="bias_raw")
+        nc.vector.memset(bias_raw[:], 0.0)
 
         ident_f = const.tile([P, P], F32, name="ident_f")
         masks.make_identity(nc, ident_f[:])
@@ -66,8 +69,6 @@ def tile_st_hmr_pb_kernel(tc, h_new, c_new, g_t, c_g_t, Wg_t, Zg_t_bytes, Zg_t_s
             out=perm_b[:].rearrange("p (t r n) -> p t r n", t=4, r=4),
             in_=ident_b[:].rearrange("p (r t n) -> p t r n", r=4, t=4),
         )
-        bias_raw = const.tile([P, P], BF16, name="bias_raw")
-        nc.vector.memset(bias_raw[:], 0.0)
 
         zs = const.tile([P, 4], F32, name="zs")
         nc.sync.dma_start(out=zs[:], in_=Zg_t_scale.rearrange("a b (p j) c -> p (a b j c)", j=4))
@@ -75,55 +76,85 @@ def tile_st_hmr_pb_kernel(tc, h_new, c_new, g_t, c_g_t, Wg_t, Zg_t_bytes, Zg_t_s
         wraw = {}
         zraw = {}
 
-        def load_unit(u):
+        def load_z(u):
             g, t = units[u]
             zraw[u] = zpool.tile([P, 4, H], U8, name="zraw", tag="zraw")
             nc.sync.dma_start(out=zraw[u][:], in_=Zg_t_bytes[g, t].rearrange("(p j) n -> p j n", j=4))
+
+        def load_w(u):
+            g, t = units[u]
             wraw[u] = wpool.tile([P, 4, H], BF16, name="wraw", tag="wraw")
             nc.sync.dma_start(out=wraw[u][:], in_=Wg_t[g, t].rearrange("(p j) n -> p j n", j=4))
 
-        load_unit(0)
+        load_z(0)
+        load_w(0)
+        load_z(1)
+        load_w(1)
         h_sb = []
         for q in range(4):
             hq = const.tile([P, 2, H], BF16, name="h_sb%d" % q)
             nc.sync.dma_start(out=hq[:], in_=h_rows[:, 2 * q : 2 * q + 2, :])
             h_sb.append(hq)
+        load_z(2)
+        load_w(2)
         g_sb = const.tile([P, 2, H], BF16, name="g_sb")
         nc.sync.dma_start(out=g_sb[:], in_=g_rows)
         nc.sync.dma_start(out=bias_raw[0:48, :], in_=bg_t.rearrange("g t o (c f) -> (g t o c) f", f=P))
-        for u in range(1, 4):
-            load_unit(u)
-        cg_sb = const.tile([P, 2, H], BF16, name="cg_sb")
-        nc.sync.dma_start(out=cg_sb[:], in_=cg_rows)
-        load_unit(4)
+        load_z(3)
+        load_w(3)
         c_sb = const.tile([P, 8, H], BF16, name="c_sb")
         nc.sync.dma_start(out=c_sb[:, 0:4, :], in_=c_rows[:, 0:4, :])
         nc.sync.dma_start(out=c_sb[:, 4:8, :], in_=c_rows[:, 4:8, :])
-        for u in range(5, n_units):
-            load_unit(u)
+        for u in range(4, 7):
+            load_z(u)
+            load_w(u)
+        cg_sb = const.tile([P, 2, H], BF16, name="cg_sb")
+        nc.sync.dma_start(out=cg_sb[:], in_=cg_rows)
+        for u in range(7, n_units):
+            load_z(u)
+            load_w(u)
+
+        hg = const.tile([P, T, ROWS, 4], BF16, name="hg", align_bytes=64)
+        hg32 = hg[:].rearrange("p t r e -> p (t r e)").bitcast(F32).rearrange("p (t r u) -> p t r u", t=T, u=2)
+        gg = const.tile([P, ROWS, 4], BF16, name="gg", align_bytes=64)
+        gg32 = gg[:].rearrange("p r e -> p (r e)").bitcast(F32).rearrange("p (i r u) -> p i r u", i=2, u=2)
+        bias_sb = const.tile([P, 48], F32, name="bias_sb")
+        h_codes = const.tile([P, T * ROWS], U32, name="h_codes", align_bytes=64)
+        h_scales = const.tile([P, T * ROWS], U8, name="h_scales", align_bytes=64)
+        g_codes = const.tile([P, ROWS], U32, name="g_codes", align_bytes=64)
+        g_scales = const.tile([P, ROWS], U8, name="g_scales", align_bytes=64)
+        tmp = const.tile([P, 2, H], F32, name="tmp")
+        cout = const.tile([P, 2, H], F32, name="cout")
+        th = const.tile([P, 2, H], F32, name="th")
+        gout = const.tile([P, 2, H], F32, name="gout")
 
         zwide = {}
         grouped = {}
         codes = {}
         scales = {}
+        banks = {}
+        sig = {}
 
-        def widen(u):
+        def widen(u, planes_on_vector):
             zwide[u] = zwpool.tile([P, 4, H], BF16, name="zwide", tag="zwide")
             for j in range(4):
-                nc.scalar.activation(
-                    out=zwide[u][:, j, :],
-                    in_=zraw[u][:, j, :].bitcast(FP8),
-                    func=ACT.Copy,
-                    scale=zs[:, j : j + 1],
-                )
+                src = zraw[u][:, j, :].bitcast(FP8)
+                if j >= 4 - planes_on_vector:
+                    nc.vector.tensor_scalar(
+                        out=zwide[u][:, j, :], in0=src, scalar1=zs[:, j : j + 1], scalar2=None, op0=ALU.mult
+                    )
+                else:
+                    nc.scalar.activation(out=zwide[u][:, j, :], in_=src, func=ACT.Copy, scale=zs[:, j : j + 1])
+
+        def interleave_scalar(u):
+            grouped[u] = gpool.tile([P, 2, H, 4], BF16, name="grouped", tag="grouped", align_bytes=64)
+            nc.scalar.copy(out=grouped[u][:, 1, 0:CZ, :], in_=zwide[u][:, :, 0:CZ].rearrange("p j n -> p n j"))
 
         def interleave_w(u):
-            grouped[u] = gpool.tile([P, 2, H, 4], BF16, name="grouped", tag="grouped", align_bytes=64)
             nc.vector.tensor_copy(out=grouped[u][:, 0, :, :], in_=wraw[u][:].rearrange("p j n -> p n j"))
 
         def interleave_z(u):
-            nc.scalar.copy(out=grouped[u][:, 1, 0:CS, :], in_=zwide[u][:, :, 0:CS].rearrange("p j n -> p n j"))
-            nc.vector.tensor_copy(out=grouped[u][:, 1, CS:H, :], in_=zwide[u][:, :, CS:H].rearrange("p j n -> p n j"))
+            nc.vector.tensor_copy(out=grouped[u][:, 1, CZ:H, :], in_=zwide[u][:, :, CZ:H].rearrange("p j n -> p n j"))
 
         def quantize(u):
             codes[u] = qpool.tile([P, 2 * H], U32, name="codes", tag="codes", align_bytes=64)
@@ -134,152 +165,244 @@ def tile_st_hmr_pb_kernel(tc, h_new, c_new, g_t, c_g_t, Wg_t, Zg_t_bytes, Zg_t_s
                 in_=grouped[u][:].rearrange("p a n j -> p (a n j)"),
             )
 
-        widen(0)
-        interleave_w(0)
-        interleave_z(0)
-        widen(1)
-
-        hg = const.tile([P, T, ROWS, 4], BF16, name="hg", align_bytes=64)
-        hg32 = hg[:].rearrange("p t r e -> p (t r e)").bitcast(F32).rearrange("p (t r u) -> p t r u", t=T, u=2)
-        for q in range(4):
-            xt = psum_mm.tile([P, 2, 2, P], F32, name="xt", tag="mm")
-            for i2 in range(2):
-                words = h_sb[q][:, i2, :].bitcast(F32)
-                for u2 in range(2):
-                    nc.tensor.transpose(out=xt[:, i2, u2, :], in_=words[:, u2::2], identity=perm_f[:])
-            for i2 in range(2):
-                i = 2 * q + i2
-                nc.scalar.copy(
-                    out=hg32[:, :, 32 * i : 32 * i + 32, :],
-                    in_=xt[:, i2, :, :].rearrange("p u (t r) -> p t r u", t=T),
-                )
-        gg = const.tile([P, ROWS, 4], BF16, name="gg", align_bytes=64)
-        gg32 = gg[:].rearrange("p r e -> p (r e)").bitcast(F32).rearrange("p (i r u) -> p i r u", i=2, u=2)
-        xg = psum_mm.tile([P, 2, 2, P], F32, name="xg", tag="mm")
-        for i2 in range(2):
-            words = g_sb[:, i2, :].bitcast(F32)
-            for u2 in range(2):
-                nc.tensor.transpose(out=xg[:, i2, u2, :], in_=words[:, u2::2], identity=ident_f[:])
-        nc.scalar.copy(out=gg32, in_=xg[:].rearrange("p i u r -> p i r u"))
-
-        bT = psum_tr.tile([P, P], BF16, name="bT", tag="tr")
-        nc.tensor.transpose(out=bT[:], in_=bias_raw[:], identity=ident_b[:])
-        bias_sb = const.tile([P, 48], F32, name="bias_sb")
-        nc.vector.tensor_copy(out=bias_sb[:], in_=bT[:, 0:48])
-
-        h_codes = const.tile([P, T * ROWS], U32, name="h_codes", align_bytes=64)
-        h_scales = const.tile([P, T * ROWS], U8, name="h_scales", align_bytes=64)
-        g_codes = const.tile([P, ROWS], U32, name="g_codes", align_bytes=64)
-        g_scales = const.tile([P, ROWS], U8, name="g_scales", align_bytes=64)
-
-        tmp = const.tile([P, 2, H], F32, name="tmp")
-        cout = const.tile([P, 2, H], F32, name="cout")
-        th = const.tile([P, 2, H], F32, name="th")
-        gout = const.tile([P, 2, H], F32, name="gout")
-
-        sig = {}
+        def gate_pair(out, u, w_cols, z_cols):
+            t = units[u][1]
+            nc.tensor.matmul_mx(
+                out=out,
+                lhsT=codes[u][:, w_cols].bitcast(FP8X4),
+                lhsT_scale=scales[u][:, w_cols],
+                rhs=h_codes[:, t * ROWS : (t + 1) * ROWS].bitcast(FP8X4),
+                rhs_scale=h_scales[:, t * ROWS : (t + 1) * ROWS],
+                start=True,
+                stop=False,
+            )
+            nc.tensor.matmul_mx(
+                out=out,
+                lhsT=codes[u][:, z_cols].bitcast(FP8X4),
+                lhsT_scale=scales[u][:, z_cols],
+                rhs=g_codes[:].bitcast(FP8X4),
+                rhs_scale=g_scales[:],
+                start=False,
+                stop=True,
+            )
 
         def multiply(u):
-            g, t = units[u]
-            banks = []
+            banks[u] = []
             for b in range(2):
                 mm = psum_mm.tile([P, 2, ROWS], F32, name="mm", tag="mm")
                 for f2 in range(2):
                     ft = 2 * b + f2
-                    w_cols = slice(ft * P, (ft + 1) * P)
-                    z_cols = slice(H + ft * P, H + (ft + 1) * P)
-                    nc.tensor.matmul_mx(
-                        out=mm[:, f2, :],
-                        lhsT=codes[u][:, w_cols].bitcast(FP8X4),
-                        lhsT_scale=scales[u][:, w_cols],
-                        rhs=h_codes[:, t * ROWS : (t + 1) * ROWS].bitcast(FP8X4),
-                        rhs_scale=h_scales[:, t * ROWS : (t + 1) * ROWS],
-                        start=True,
-                        stop=False,
-                    )
-                    nc.tensor.matmul_mx(
-                        out=mm[:, f2, :],
-                        lhsT=codes[u][:, z_cols].bitcast(FP8X4),
-                        lhsT_scale=scales[u][:, z_cols],
-                        rhs=g_codes[:].bitcast(FP8X4),
-                        rhs_scale=g_scales[:],
-                        start=False,
-                        stop=True,
-                    )
-                banks.append(mm)
+                    gate_pair(mm[:, f2, :], u, slice(ft * P, (ft + 1) * P), slice(H + ft * P, H + (ft + 1) * P))
+                banks[u].append(mm)
+
+        def sigmoid_one(u, ft, src):
+            g, t = units[u]
+            col = (g * T + t) * NFT + ft
+            nc.scalar.activation(out=sig[g][:, ft, t, :], in_=src, func=ACT.Sigmoid, bias=bias_sb[:, col : col + 1])
+
+        def sigmoid(u):
+            g, t = units[u]
             if t == 0:
                 sig[g] = spool.tile([P, NFT, T, ROWS], F32, name="sig", tag="sig")
-            for b in range(2):
-                for f2 in range(2):
-                    ft = 2 * b + f2
-                    col = (g * T + t) * NFT + ft
-                    nc.scalar.activation(
-                        out=sig[g][:, ft, t, :],
-                        in_=banks[b][:, f2, :],
-                        func=ACT.Sigmoid,
-                        bias=bias_sb[:, col : col + 1],
-                    )
+            for ft in range(NFT):
+                sigmoid_one(u, ft, banks[u][ft // 2][:, ft % 2, :])
 
-        def sum_frames(g):
+        def sum_group(out, g, ft, rt):
+            for t in range(T):
+                nc.tensor.matmul(
+                    out=out,
+                    lhsT=sig[g][:, ft, t, rt * P : (rt + 1) * P],
+                    rhs=ident_f[:],
+                    is_transpose=True,
+                    start=(t == 0),
+                    stop=(t == T - 1),
+                )
+
+        def sum_frames(g, pool, tag):
             accs = []
             for rt in range(2):
-                acc = psum_acc.tile([P, H], F32, name="acc", tag="acc")
+                acc = pool.tile([P, H], F32, name="acc_" + tag, tag=tag)
                 for ft in range(NFT):
-                    for t in range(T):
-                        nc.tensor.matmul(
-                            out=acc[:, ft * P : (ft + 1) * P],
-                            lhsT=sig[g][:, ft, t, rt * P : (rt + 1) * P],
-                            rhs=ident_f[:],
-                            is_transpose=True,
-                            start=(t == 0),
-                            stop=(t == T - 1),
-                        )
+                    sum_group(acc[:, ft * P : (ft + 1) * P], g, ft, rt)
                 accs.append(acc)
             return accs
 
-        def gate_end(g):
-            if g == 0:
-                for ft in range(NFT):
-                    cT = psum_tr.tile([P, 8, P], BF16, name="cT", tag="tr")
-                    for i in range(8):
-                        nc.tensor.transpose(out=cT[:, i, :], in_=c_sb[:, i, ft * P : (ft + 1) * P], identity=perm_b[:])
-                    view = sig[g][:, ft, :, :].rearrange("p t (i r) -> p t i r", i=8)
-                    nc.vector.tensor_tensor(
-                        out=view, in0=view, in1=cT[:].rearrange("p i (t r) -> p t i r", t=T), op=ALU.mult
-                    )
-            accs = sum_frames(g)
-            for rt in range(2):
-                if g == 1:
-                    nc.vector.scalar_tensor_tensor(
-                        out=tmp[:, rt, :], in0=accs[rt][:], scalar=0.25, in1=cg_sb[:, rt, :], op0=ALU.mult, op1=ALU.mult
-                    )
-                elif g == 0:
-                    nc.vector.scalar_tensor_tensor(
-                        out=cout[:, rt, :], in0=accs[rt][:], scalar=0.25, in1=tmp[:, rt, :], op0=ALU.mult, op1=ALU.add
-                    )
-                    nc.sync.dma_start(out=out1_rows[:, rt, :], in_=cout[:, rt, :])
-                    nc.scalar.activation(out=th[:, rt, :], in_=cout[:, rt, :], func=ACT.Tanh)
-                else:
-                    nc.vector.scalar_tensor_tensor(
-                        out=gout[:, rt, :], in0=accs[rt][:], scalar=0.25, in1=th[:, rt, :], op0=ALU.mult, op1=ALU.mult
-                    )
-                    nc.sync.dma_start(out=out0_rows[:, rt, :], in_=gout[:, rt, :])
+        cts = {}
 
-        for u in range(n_units):
-            if u + 2 < n_units:
-                widen(u + 2)
-            if u + 1 < n_units:
-                interleave_w(u + 1)
-            quantize(u)
-            if u == 0:
+        def turn_c(ft):
+            cts[ft] = psum_tr.tile([P, 8, P], BF16, name="cT", tag="tr")
+            for i in range(8):
+                nc.tensor.transpose(out=cts[ft][:, i, :], in_=c_sb[:, i, ft * P : (ft + 1) * P], identity=perm_b[:])
+
+        def times_c(ft):
+            view = sig[0][:, ft, :, :].rearrange("p t (i r) -> p t i r", i=8)
+            nc.vector.tensor_tensor(out=view, in0=view, in1=cts[ft][:].rearrange("p i (t r) -> p t i r", t=T), op=ALU.mult)
+
+        xts = {}
+
+        def turn_h(q):
+            xts[q] = psum_mm.tile([P, 2, 2, P], F32, name="xt", tag="mm")
+            for i2 in range(2):
+                words = h_sb[q][:, i2, :].bitcast(F32)
+                for u2 in range(2):
+                    nc.tensor.transpose(out=xts[q][:, i2, u2, :], in_=words[:, u2::2], identity=perm_f[:])
+
+        def h_out(q, engine_copy):
+            for i2 in range(2):
+                i = 2 * q + i2
+                engine_copy(
+                    out=hg32[:, :, 32 * i : 32 * i + 32, :],
+                    in_=xts[q][:, i2, :, :].rearrange("p u (t r) -> p t r u", t=T),
+                )
+
+        f_acc = None
+        g_acc = None
+
+        for s in range(n_units):
+            a = s - 1
+            b = s - 2
+            c = s - 3
+            if a >= 0:
+                interleave_scalar(a)
+                interleave_w(a)
+            if s == 1:
+                for q in range(4):
+                    turn_h(q)
+            if s == 2:
+                h_out(0, nc.scalar.copy)
+                h_out(1, nc.scalar.copy)
+            if s == 3:
                 nc.vector.quantize_mx(
                     out=h_codes[:].bitcast(FP8X4), scales=h_scales[:], in_=hg[:].rearrange("p t r e -> p (t r e)")
                 )
+                nc.vector.tensor_copy(out=gg32, in_=xg[:].rearrange("p i u r -> p i r u"))
+            if b >= 0:
+                quantize(b)
+            if s == 3:
                 nc.vector.quantize_mx(
                     out=g_codes[:].bitcast(FP8X4), scales=g_scales[:], in_=gg[:].rearrange("p r e -> p (r e)")
                 )
-            if u + 1 < n_units:
-                interleave_z(u + 1)
-            multiply(u)
-            if units[u][1] == T - 1:
-                gate_end(units[u][0])
+            if a >= 0:
+                interleave_z(a)
+            if s == 2:
+                h_out(2, nc.vector.tensor_copy)
+                h_out(3, nc.vector.tensor_copy)
+                xg = psum_mm.tile([P, 2, 2, P], F32, name="xg", tag="mm")
+                for i2 in range(2):
+                    words = g_sb[:, i2, :].bitcast(F32)
+                    for u2 in range(2):
+                        nc.tensor.transpose(out=xg[:, i2, u2, :], in_=words[:, u2::2], identity=ident_f[:])
+                bT = psum_tr.tile([P, P], BF16, name="bT", tag="tr")
+                nc.tensor.transpose(out=bT[:], in_=bias_raw[:], identity=ident_b[:])
+            if s == 3:
+                nc.vector.tensor_copy(out=bias_sb[:], in_=bT[:, 0:48])
+            if s == 7:
+                times_c(0)
+                times_c(1)
+            if s == 8:
+                times_c(2)
+                times_c(3)
+            widen(s, 2 if s == 0 else 0)
+            if s == 3:
+                multiply(0)
+            if b >= 1:
+                multiply(b)
+            if s == 5:
+                turn_c(0)
+                turn_c(1)
+            if s == 7:
+                turn_c(2)
+                turn_c(3)
+            if s == 9:
+                f_acc = sum_frames(0, psum_acc, "acc")
+            if s == 11:
+                g_acc = sum_frames(1, psum_tr, "tr")
+            if c >= 0:
+                sigmoid(c)
+
+        grp = gpool.tile([P, NFT, 2, P, 4], BF16, name="grp", tag="grouped", align_bytes=64)
+        codes[last] = qpool.tile([P, 2 * H], U32, name="codes_l", tag="codes", align_bytes=64)
+        scales[last] = qpool.tile([P, 2 * H], U8, name="scales_l", tag="scales", align_bytes=64)
+
+        def chunk_w(ft):
+            nc.vector.tensor_copy(
+                out=grp[:, ft, 0, :, :], in_=wraw[last][:, :, ft * P : (ft + 1) * P].rearrange("p j n -> p n j")
+            )
+
+        def chunk_z(ft, engine_copy):
+            engine_copy(out=grp[:, ft, 1, :, :], in_=zwide[last][:, :, ft * P : (ft + 1) * P].rearrange("p j n -> p n j"))
+
+        def chunk_q(ft):
+            nc.vector.quantize_mx(
+                out=codes[last][:, ft * 2 * P : (ft + 1) * 2 * P].bitcast(FP8X4),
+                scales=scales[last][:, ft * 2 * P : (ft + 1) * 2 * P],
+                in_=grp[:, ft, :, :, :].rearrange("p a n j -> p (a n j)"),
+            )
+
+        chunk_mm = {}
+
+        def chunk_multiply(ft):
+            chunk_mm[ft] = psum_mm.tile([P, 2, ROWS], F32, name="mm_l", tag="mm")
+            base = ft * 2 * P
+            gate_pair(chunk_mm[ft][:, 0, :], last, slice(base, base + P), slice(base + P, base + 2 * P))
+
+        o_acc = {}
+
+        def chunk_sum(ft):
+            if ft < 2:
+                o_acc[ft] = psum_tr.tile([P, 2, P], F32, name="o_acc_a", tag="tr")
+            else:
+                o_acc[ft] = psum_acc.tile([P, 2, P], F32, name="o_acc_b", tag="acc")
+            for rt in range(2):
+                sum_group(o_acc[ft][:, rt, :], 2, ft, rt)
+
+        def chunk_out(ft):
+            cols = slice(ft * P, (ft + 1) * P)
+            nc.vector.scalar_tensor_tensor(
+                out=gout[:, :, cols], in0=o_acc[ft][:], scalar=0.25, in1=th[:, :, cols], op0=ALU.mult, op1=ALU.mult
+            )
+            nc.sync.dma_start(out=out0_rows[:, :, cols], in_=gout[:, :, cols])
+
+        chunk_z(2, nc.scalar.copy)
+        chunk_z(3, nc.scalar.copy)
+        sigmoid(last - 2)
+
+        chunk_w(0)
+        chunk_z(0, nc.vector.tensor_copy)
+        quantize(last - 1)
+        multiply(last - 1)
+        for rt in range(2):
+            nc.vector.scalar_tensor_tensor(
+                out=tmp[:, rt, :], in0=g_acc[rt][:], scalar=0.25, in1=cg_sb[:, rt, :], op0=ALU.mult, op1=ALU.mult
+            )
+        chunk_w(1)
+        chunk_z(1, nc.vector.tensor_copy)
+        chunk_q(0)
+        chunk_multiply(0)
+        sigmoid(last - 1)
+        sigmoid_one(last, 0, chunk_mm[0][:, 0, :])
+        for rt in range(2):
+            nc.vector.scalar_tensor_tensor(
+                out=cout[:, rt, :], in0=f_acc[rt][:], scalar=0.25, in1=tmp[:, rt, :], op0=ALU.mult, op1=ALU.add
+            )
+            nc.sync.dma_start(out=out1_rows[:, rt, :], in_=cout[:, rt, :])
+            nc.scalar.activation(out=th[:, rt, :], in_=cout[:, rt, :], func=ACT.Tanh)
+        chunk_w(2)
+        chunk_q(1)
+        chunk_multiply(1)
+        chunk_sum(0)
+        sigmoid_one(last, 1, chunk_mm[1][:, 0, :])
+        chunk_w(3)
+        chunk_q(2)
+        chunk_multiply(2)
+        chunk_sum(1)
+        sigmoid_one(last, 2, chunk_mm[2][:, 0, :])
+        chunk_q(3)
+        chunk_multiply(3)
+        chunk_sum(2)
+        sigmoid_one(last, 3, chunk_mm[3][:, 0, :])
+        chunk_out(0)
+        chunk_out(1)
+        chunk_sum(3)
+        chunk_out(2)
+        chunk_out(3)

@@ -19,7 +19,8 @@ H = 512
 T = 4
 ROWS = 256
 NFT = 4
-CZ = 96
+ROUTED = 256
+N_ROUTED = 8
 
 
 def tile_st_hmr_pb_kernel(tc, h_new, c_new, g_t, c_g_t, Wg_t, Zg_t_bytes, Zg_t_scale, bg_t, out_0, out_1):
@@ -37,9 +38,8 @@ def tile_st_hmr_pb_kernel(tc, h_new, c_new, g_t, c_g_t, Wg_t, Zg_t_bytes, Zg_t_s
 
     with ExitStack() as ctx:
         const = ctx.enter_context(tc.tile_pool(name="const", bufs=1))
-        wpool = ctx.enter_context(tc.tile_pool(name="wpool", bufs=8))
+        xpool = ctx.enter_context(tc.tile_pool(name="xpool", bufs=6))
         zpool = ctx.enter_context(tc.tile_pool(name="zpool", bufs=8))
-        zwpool = ctx.enter_context(tc.tile_pool(name="zwpool", bufs=3))
         gpool = ctx.enter_context(tc.tile_pool(name="gpool", bufs=3))
         qpool = ctx.enter_context(tc.tile_pool(name="qpool", bufs=4))
         spool = ctx.enter_context(tc.tile_pool(name="spool", bufs=2))
@@ -73,7 +73,7 @@ def tile_st_hmr_pb_kernel(tc, h_new, c_new, g_t, c_g_t, Wg_t, Zg_t_bytes, Zg_t_s
         zs = const.tile([P, 4], F32, name="zs")
         nc.sync.dma_start(out=zs[:], in_=Zg_t_scale.rearrange("a b (p j) c -> p (a b j c)", j=4))
 
-        wraw = {}
+        planes = {}
         zraw = {}
 
         def load_z(u):
@@ -83,8 +83,8 @@ def tile_st_hmr_pb_kernel(tc, h_new, c_new, g_t, c_g_t, Wg_t, Zg_t_bytes, Zg_t_s
 
         def load_w(u):
             g, t = units[u]
-            wraw[u] = wpool.tile([P, 4, H], BF16, name="wraw", tag="wraw")
-            nc.sync.dma_start(out=wraw[u][:], in_=Wg_t[g, t].rearrange("(p j) n -> p j n", j=4))
+            planes[u] = xpool.tile([P, 4, 2, H], BF16, name="planes", tag="planes")
+            nc.sync.dma_start(out=planes[u][:, :, 0, :], in_=Wg_t[g, t].rearrange("(p j) n -> p j n", j=4))
 
         load_z(0)
         load_w(0)
@@ -128,7 +128,7 @@ def tile_st_hmr_pb_kernel(tc, h_new, c_new, g_t, c_g_t, Wg_t, Zg_t_bytes, Zg_t_s
         th = const.tile([P, 2, H], F32, name="th")
         gout = const.tile([P, 2, H], F32, name="gout")
 
-        zwide = {}
+        routed = {}
         grouped = {}
         codes = {}
         scales = {}
@@ -136,25 +136,42 @@ def tile_st_hmr_pb_kernel(tc, h_new, c_new, g_t, c_g_t, Wg_t, Zg_t_bytes, Zg_t_s
         sig = {}
 
         def widen(u, planes_on_vector):
-            zwide[u] = zwpool.tile([P, 4, H], BF16, name="zwide", tag="zwide")
             for j in range(4):
                 src = zraw[u][:, j, :].bitcast(FP8)
                 if j >= 4 - planes_on_vector:
                     nc.vector.tensor_scalar(
-                        out=zwide[u][:, j, :], in0=src, scalar1=zs[:, j : j + 1], scalar2=None, op0=ALU.mult
+                        out=planes[u][:, j, 1, :], in0=src, scalar1=zs[:, j : j + 1], scalar2=None, op0=ALU.mult
                     )
                 else:
-                    nc.scalar.activation(out=zwide[u][:, j, :], in_=src, func=ACT.Copy, scale=zs[:, j : j + 1])
+                    nc.scalar.activation(out=planes[u][:, j, 1, :], in_=src, func=ACT.Copy, scale=zs[:, j : j + 1])
 
-        def interleave_scalar(u):
-            grouped[u] = gpool.tile([P, 2, H, 4], BF16, name="grouped", tag="grouped", align_bytes=64)
-            nc.scalar.copy(out=grouped[u][:, 1, 0:CZ, :], in_=zwide[u][:, :, 0:CZ].rearrange("p j n -> p n j"))
+        def route(u):
+            routed[u] = psum_acc.tile([P, 4 * ROUTED], BF16, name="routed", tag="acc")
+            for half in range(2):
+                nc.tensor.matmul(
+                    out=routed[u][:].rearrange("p (n k e) -> p k n e", k=2, e=2)[:, half, :, :],
+                    lhsT=ident_b[:],
+                    rhs=planes[u][:, 2 * half : 2 * half + 2, 0, 0:ROUTED].rearrange("p e n -> p n e"),
+                    start=True,
+                    stop=True,
+                )
 
-        def interleave_w(u):
-            nc.vector.tensor_copy(out=grouped[u][:, 0, :, :], in_=wraw[u][:].rearrange("p j n -> p n j"))
+        def weave(engine_copy, dst, src):
+            engine_copy(
+                out=dst.rearrange("p (c i) t -> p c t i", i=4), in_=src.rearrange("p t (c i) -> p c t i", i=4)
+            )
 
-        def interleave_z(u):
-            nc.vector.tensor_copy(out=grouped[u][:, 1, CZ:H, :], in_=zwide[u][:, :, CZ:H].rearrange("p j n -> p n j"))
+        def interleave(u):
+            grouped[u] = gpool.tile([P, 2 * H, 4], BF16, name="grouped", tag="grouped", align_bytes=64)
+            first = 0
+            if u < N_ROUTED:
+                first = ROUTED
+                nc.scalar.copy(out=grouped[u][:, 0:ROUTED, :].rearrange("p n j -> p (n j)"), in_=routed[u][:])
+            weave(
+                nc.vector.tensor_copy,
+                grouped[u][:, first : 2 * H, :],
+                planes[u][:].rearrange("p j a n -> p j (a n)")[:, :, first : 2 * H],
+            )
 
         def quantize(u):
             codes[u] = qpool.tile([P, 2 * H], U32, name="codes", tag="codes", align_bytes=64)
@@ -162,7 +179,7 @@ def tile_st_hmr_pb_kernel(tc, h_new, c_new, g_t, c_g_t, Wg_t, Zg_t_bytes, Zg_t_s
             nc.vector.quantize_mx(
                 out=codes[u][:].bitcast(FP8X4),
                 scales=scales[u][:],
-                in_=grouped[u][:].rearrange("p a n j -> p (a n j)"),
+                in_=grouped[u][:].rearrange("p n j -> p (n j)"),
             )
 
         def gate_pair(out, u, w_cols, z_cols):
@@ -262,9 +279,10 @@ def tile_st_hmr_pb_kernel(tc, h_new, c_new, g_t, c_g_t, Wg_t, Zg_t_bytes, Zg_t_s
             a = s - 1
             b = s - 2
             c = s - 3
+            if s < N_ROUTED:
+                route(s)
             if a >= 0:
-                interleave_scalar(a)
-                interleave_w(a)
+                interleave(a)
             if s == 1:
                 for q in range(4):
                     turn_h(q)
@@ -282,8 +300,6 @@ def tile_st_hmr_pb_kernel(tc, h_new, c_new, g_t, c_g_t, Wg_t, Zg_t_bytes, Zg_t_s
                 nc.vector.quantize_mx(
                     out=g_codes[:].bitcast(FP8X4), scales=g_scales[:], in_=gg[:].rearrange("p r e -> p (r e)")
                 )
-            if a >= 0:
-                interleave_z(a)
             if s == 2:
                 h_out(2, nc.vector.tensor_copy)
                 h_out(3, nc.vector.tensor_copy)
@@ -325,12 +341,10 @@ def tile_st_hmr_pb_kernel(tc, h_new, c_new, g_t, c_g_t, Wg_t, Zg_t_bytes, Zg_t_s
         scales[last] = qpool.tile([P, 2 * H], U8, name="scales_l", tag="scales", align_bytes=64)
 
         def chunk_w(ft):
-            nc.vector.tensor_copy(
-                out=grp[:, ft, 0, :, :], in_=wraw[last][:, :, ft * P : (ft + 1) * P].rearrange("p j n -> p n j")
-            )
+            weave(nc.vector.tensor_copy, grp[:, ft, 0, :, :], planes[last][:, :, 0, ft * P : (ft + 1) * P])
 
         def chunk_z(ft, engine_copy):
-            engine_copy(out=grp[:, ft, 1, :, :], in_=zwide[last][:, :, ft * P : (ft + 1) * P].rearrange("p j n -> p n j"))
+            weave(engine_copy, grp[:, ft, 1, :, :], planes[last][:, :, 1, ft * P : (ft + 1) * P])
 
         def chunk_q(ft):
             nc.vector.quantize_mx(

@@ -20,7 +20,11 @@ T = 4
 ROWS = 256
 NFT = 4
 ROUTED = 256
-N_ROUTED = 8
+RT = [1, 1, 1, 1, 1, 1, 1, 1, 1, 0, 0, 0]
+SH = [0, 0, 0, 0, 0, 0, 0, 0, 0, 128, 128, 0]
+NV = [1, 1, 1, 1, 1, 1, 0, 0, 0, 0, 0, 0]
+ZL = 0
+HS = 4
 
 
 def tile_st_hmr_pb_kernel(tc, h_new, c_new, g_t, c_g_t, Wg_t, Zg_t_bytes, Zg_t_scale, bg_t, out_0, out_1):
@@ -38,8 +42,9 @@ def tile_st_hmr_pb_kernel(tc, h_new, c_new, g_t, c_g_t, Wg_t, Zg_t_bytes, Zg_t_s
 
     with ExitStack() as ctx:
         const = ctx.enter_context(tc.tile_pool(name="const", bufs=1))
-        xpool = ctx.enter_context(tc.tile_pool(name="xpool", bufs=6))
+        wpool = ctx.enter_context(tc.tile_pool(name="wpool", bufs=8))
         zpool = ctx.enter_context(tc.tile_pool(name="zpool", bufs=8))
+        zwpool = ctx.enter_context(tc.tile_pool(name="zwpool", bufs=3 + ZL))
         gpool = ctx.enter_context(tc.tile_pool(name="gpool", bufs=3))
         qpool = ctx.enter_context(tc.tile_pool(name="qpool", bufs=4))
         spool = ctx.enter_context(tc.tile_pool(name="spool", bufs=2))
@@ -73,7 +78,7 @@ def tile_st_hmr_pb_kernel(tc, h_new, c_new, g_t, c_g_t, Wg_t, Zg_t_bytes, Zg_t_s
         zs = const.tile([P, 4], F32, name="zs")
         nc.sync.dma_start(out=zs[:], in_=Zg_t_scale.rearrange("a b (p j) c -> p (a b j c)", j=4))
 
-        planes = {}
+        wraw = {}
         zraw = {}
 
         def load_z(u):
@@ -83,8 +88,8 @@ def tile_st_hmr_pb_kernel(tc, h_new, c_new, g_t, c_g_t, Wg_t, Zg_t_bytes, Zg_t_s
 
         def load_w(u):
             g, t = units[u]
-            planes[u] = xpool.tile([P, 4, 2, H], BF16, name="planes", tag="planes")
-            nc.sync.dma_start(out=planes[u][:, :, 0, :], in_=Wg_t[g, t].rearrange("(p j) n -> p j n", j=4))
+            wraw[u] = wpool.tile([P, 4, H], BF16, name="wraw", tag="wraw")
+            nc.sync.dma_start(out=wraw[u][:], in_=Wg_t[g, t].rearrange("(p j) n -> p j n", j=4))
 
         load_z(0)
         load_w(0)
@@ -128,6 +133,7 @@ def tile_st_hmr_pb_kernel(tc, h_new, c_new, g_t, c_g_t, Wg_t, Zg_t_bytes, Zg_t_s
         th = const.tile([P, 2, H], F32, name="th")
         gout = const.tile([P, 2, H], F32, name="gout")
 
+        zwide = {}
         routed = {}
         grouped = {}
         codes = {}
@@ -136,14 +142,15 @@ def tile_st_hmr_pb_kernel(tc, h_new, c_new, g_t, c_g_t, Wg_t, Zg_t_bytes, Zg_t_s
         sig = {}
 
         def widen(u, planes_on_vector):
+            zwide[u] = zwpool.tile([P, 4, H], BF16, name="zwide", tag="zwide")
             for j in range(4):
                 src = zraw[u][:, j, :].bitcast(FP8)
                 if j >= 4 - planes_on_vector:
                     nc.vector.tensor_scalar(
-                        out=planes[u][:, j, 1, :], in0=src, scalar1=zs[:, j : j + 1], scalar2=None, op0=ALU.mult
+                        out=zwide[u][:, j, :], in0=src, scalar1=zs[:, j : j + 1], scalar2=None, op0=ALU.mult
                     )
                 else:
-                    nc.scalar.activation(out=planes[u][:, j, 1, :], in_=src, func=ACT.Copy, scale=zs[:, j : j + 1])
+                    nc.scalar.activation(out=zwide[u][:, j, :], in_=src, func=ACT.Copy, scale=zs[:, j : j + 1])
 
         def route(u):
             routed[u] = psum_acc.tile([P, 4 * ROUTED], BF16, name="routed", tag="acc")
@@ -151,27 +158,28 @@ def tile_st_hmr_pb_kernel(tc, h_new, c_new, g_t, c_g_t, Wg_t, Zg_t_bytes, Zg_t_s
                 nc.tensor.matmul(
                     out=routed[u][:].rearrange("p (n k e) -> p k n e", k=2, e=2)[:, half, :, :],
                     lhsT=ident_b[:],
-                    rhs=planes[u][:, 2 * half : 2 * half + 2, 0, 0:ROUTED].rearrange("p e n -> p n e"),
+                    rhs=wraw[u][:, 2 * half : 2 * half + 2, 0:ROUTED].rearrange("p e n -> p n e"),
                     start=True,
                     stop=True,
                 )
 
-        def weave(engine_copy, dst, src):
-            engine_copy(
-                out=dst.rearrange("p (c i) t -> p c t i", i=4), in_=src.rearrange("p t (c i) -> p c t i", i=4)
-            )
+        def interleave_scalar(u):
+            grouped[u] = gpool.tile([P, 2, H, 4], BF16, name="grouped", tag="grouped", align_bytes=64)
+            lo = 0
+            if RT[u]:
+                lo = ROUTED
+                nc.scalar.copy(out=grouped[u][:, 0, 0:ROUTED, :].rearrange("p n j -> p (n j)"), in_=routed[u][:])
+            if SH[u]:
+                nc.scalar.copy(
+                    out=grouped[u][:, 0, lo : lo + SH[u], :], in_=wraw[u][:, :, lo : lo + SH[u]].rearrange("p j n -> p n j")
+                )
 
-        def interleave(u):
-            grouped[u] = gpool.tile([P, 2 * H, 4], BF16, name="grouped", tag="grouped", align_bytes=64)
-            first = 0
-            if u < N_ROUTED:
-                first = ROUTED
-                nc.scalar.copy(out=grouped[u][:, 0:ROUTED, :].rearrange("p n j -> p (n j)"), in_=routed[u][:])
-            weave(
-                nc.vector.tensor_copy,
-                grouped[u][:, first : 2 * H, :],
-                planes[u][:].rearrange("p j a n -> p j (a n)")[:, :, first : 2 * H],
-            )
+        def interleave_w(u):
+            lo = ROUTED * RT[u] + SH[u]
+            nc.vector.tensor_copy(out=grouped[u][:, 0, lo:H, :], in_=wraw[u][:, :, lo:H].rearrange("p j n -> p n j"))
+
+        def interleave_z(u):
+            nc.vector.tensor_copy(out=grouped[u][:, 1, :, :], in_=zwide[u][:].rearrange("p j n -> p n j"))
 
         def quantize(u):
             codes[u] = qpool.tile([P, 2 * H], U32, name="codes", tag="codes", align_bytes=64)
@@ -179,7 +187,7 @@ def tile_st_hmr_pb_kernel(tc, h_new, c_new, g_t, c_g_t, Wg_t, Zg_t_bytes, Zg_t_s
             nc.vector.quantize_mx(
                 out=codes[u][:].bitcast(FP8X4),
                 scales=scales[u][:],
-                in_=grouped[u][:].rearrange("p n j -> p (n j)"),
+                in_=grouped[u][:].rearrange("p a n j -> p (a n j)"),
             )
 
         def gate_pair(out, u, w_cols, z_cols):
@@ -274,21 +282,47 @@ def tile_st_hmr_pb_kernel(tc, h_new, c_new, g_t, c_g_t, Wg_t, Zg_t_bytes, Zg_t_s
 
         f_acc = None
         g_acc = None
+        o_acc = {}
+
+        def o_sum(u, fts):
+            t = units[u][1]
+            for ft in fts:
+                if t == 0:
+                    if ft < 2:
+                        o_acc[ft] = psum_tr.tile([P, 2, P], F32, name="o_acc_a", tag="tr")
+                    else:
+                        o_acc[ft] = psum_acc.tile([P, 2, P], F32, name="o_acc_b", tag="acc")
+                for rt in range(2):
+                    nc.tensor.matmul(
+                        out=o_acc[ft][:, rt, :],
+                        lhsT=sig[2][:, ft, t, rt * P : (rt + 1) * P],
+                        rhs=ident_f[:],
+                        is_transpose=True,
+                        start=(t == 0 and rt == 0),
+                        stop=(t == T - 1 and rt == 1),
+                    )
+
+        for z in range(ZL):
+            widen(z, NV[z])
 
         for s in range(n_units):
             a = s - 1
             b = s - 2
             c = s - 3
-            if s < N_ROUTED:
+            w = s + ZL
+            if RT[s]:
                 route(s)
+            if s == 11:
+                g_acc = sum_frames(1, psum_tr, "tr")
             if a >= 0:
-                interleave(a)
+                interleave_scalar(a)
+                interleave_w(a)
             if s == 1:
                 for q in range(4):
                     turn_h(q)
             if s == 2:
-                h_out(0, nc.scalar.copy)
-                h_out(1, nc.scalar.copy)
+                for q in range(HS):
+                    h_out(q, nc.scalar.copy)
             if s == 3:
                 nc.vector.quantize_mx(
                     out=h_codes[:].bitcast(FP8X4), scales=h_scales[:], in_=hg[:].rearrange("p t r e -> p (t r e)")
@@ -300,9 +334,11 @@ def tile_st_hmr_pb_kernel(tc, h_new, c_new, g_t, c_g_t, Wg_t, Zg_t_bytes, Zg_t_s
                 nc.vector.quantize_mx(
                     out=g_codes[:].bitcast(FP8X4), scales=g_scales[:], in_=gg[:].rearrange("p r e -> p (r e)")
                 )
+            if a >= 0:
+                interleave_z(a)
             if s == 2:
-                h_out(2, nc.vector.tensor_copy)
-                h_out(3, nc.vector.tensor_copy)
+                for q in range(HS, 4):
+                    h_out(q, nc.vector.tensor_copy)
                 xg = psum_mm.tile([P, 2, 2, P], F32, name="xg", tag="mm")
                 for i2 in range(2):
                     words = g_sb[:, i2, :].bitcast(F32)
@@ -310,16 +346,26 @@ def tile_st_hmr_pb_kernel(tc, h_new, c_new, g_t, c_g_t, Wg_t, Zg_t_bytes, Zg_t_s
                         nc.tensor.transpose(out=xg[:, i2, u2, :], in_=words[:, u2::2], identity=ident_f[:])
                 bT = psum_tr.tile([P, P], BF16, name="bT", tag="tr")
                 nc.tensor.transpose(out=bT[:], in_=bias_raw[:], identity=ident_b[:])
-            if s == 3:
-                nc.vector.tensor_copy(out=bias_sb[:], in_=bT[:, 0:48])
             if s == 7:
                 times_c(0)
                 times_c(1)
             if s == 8:
                 times_c(2)
                 times_c(3)
-            widen(s, 2 if s == 0 else 0)
+            if s == 11:
+                for rt in range(2):
+                    nc.vector.scalar_tensor_tensor(
+                        out=tmp[:, rt, :], in0=g_acc[rt][:], scalar=0.25, in1=cg_sb[:, rt, :], op0=ALU.mult, op1=ALU.mult
+                    )
+                for rt in range(2):
+                    nc.vector.scalar_tensor_tensor(
+                        out=cout[:, rt, :], in0=f_acc[rt][:], scalar=0.25, in1=tmp[:, rt, :], op0=ALU.mult, op1=ALU.add
+                    )
+                    nc.sync.dma_start(out=out1_rows[:, rt, :], in_=cout[:, rt, :])
+            if w < n_units:
+                widen(w, NV[w])
             if s == 3:
+                nc.scalar.copy(out=bias_sb[:], in_=bT[:, 0:48])
                 multiply(0)
             if b >= 1:
                 multiply(b)
@@ -331,8 +377,6 @@ def tile_st_hmr_pb_kernel(tc, h_new, c_new, g_t, c_g_t, Wg_t, Zg_t_bytes, Zg_t_s
                 turn_c(3)
             if s == 9:
                 f_acc = sum_frames(0, psum_acc, "acc")
-            if s == 11:
-                g_acc = sum_frames(1, psum_tr, "tr")
             if c >= 0:
                 sigmoid(c)
 
@@ -341,10 +385,12 @@ def tile_st_hmr_pb_kernel(tc, h_new, c_new, g_t, c_g_t, Wg_t, Zg_t_bytes, Zg_t_s
         scales[last] = qpool.tile([P, 2 * H], U8, name="scales_l", tag="scales", align_bytes=64)
 
         def chunk_w(ft):
-            weave(nc.vector.tensor_copy, grp[:, ft, 0, :, :], planes[last][:, :, 0, ft * P : (ft + 1) * P])
+            nc.vector.tensor_copy(
+                out=grp[:, ft, 0, :, :], in_=wraw[last][:, :, ft * P : (ft + 1) * P].rearrange("p j n -> p n j")
+            )
 
         def chunk_z(ft, engine_copy):
-            weave(engine_copy, grp[:, ft, 1, :, :], planes[last][:, :, 1, ft * P : (ft + 1) * P])
+            engine_copy(out=grp[:, ft, 1, :, :], in_=zwide[last][:, :, ft * P : (ft + 1) * P].rearrange("p j n -> p n j"))
 
         def chunk_q(ft):
             nc.vector.quantize_mx(
@@ -360,16 +406,6 @@ def tile_st_hmr_pb_kernel(tc, h_new, c_new, g_t, c_g_t, Wg_t, Zg_t_bytes, Zg_t_s
             base = ft * 2 * P
             gate_pair(chunk_mm[ft][:, 0, :], last, slice(base, base + P), slice(base + P, base + 2 * P))
 
-        o_acc = {}
-
-        def chunk_sum(ft):
-            if ft < 2:
-                o_acc[ft] = psum_tr.tile([P, 2, P], F32, name="o_acc_a", tag="tr")
-            else:
-                o_acc[ft] = psum_acc.tile([P, 2, P], F32, name="o_acc_b", tag="acc")
-            for rt in range(2):
-                sum_group(o_acc[ft][:, rt, :], 2, ft, rt)
-
         def chunk_out(ft):
             cols = slice(ft * P, (ft + 1) * P)
             nc.vector.scalar_tensor_tensor(
@@ -377,46 +413,31 @@ def tile_st_hmr_pb_kernel(tc, h_new, c_new, g_t, c_g_t, Wg_t, Zg_t_bytes, Zg_t_s
             )
             nc.sync.dma_start(out=out0_rows[:, :, cols], in_=gout[:, :, cols])
 
+        all_ft = range(NFT)
         chunk_z(2, nc.scalar.copy)
         chunk_z(3, nc.scalar.copy)
         sigmoid(last - 2)
-
-        chunk_w(0)
-        chunk_z(0, nc.vector.tensor_copy)
+        o_sum(last - 3, all_ft)
         quantize(last - 1)
         multiply(last - 1)
+        o_sum(last - 2, all_ft)
         for rt in range(2):
-            nc.vector.scalar_tensor_tensor(
-                out=tmp[:, rt, :], in0=g_acc[rt][:], scalar=0.25, in1=cg_sb[:, rt, :], op0=ALU.mult, op1=ALU.mult
-            )
+            nc.scalar.activation(out=th[:, rt, :], in_=cout[:, rt, :], func=ACT.Tanh)
+        sigmoid(last - 1)
+        chunk_w(0)
+        chunk_z(0, nc.vector.tensor_copy)
         chunk_w(1)
         chunk_z(1, nc.vector.tensor_copy)
         chunk_q(0)
-        chunk_multiply(0)
-        sigmoid(last - 1)
-        sigmoid_one(last, 0, chunk_mm[0][:, 0, :])
-        for rt in range(2):
-            nc.vector.scalar_tensor_tensor(
-                out=cout[:, rt, :], in0=f_acc[rt][:], scalar=0.25, in1=tmp[:, rt, :], op0=ALU.mult, op1=ALU.add
-            )
-            nc.sync.dma_start(out=out1_rows[:, rt, :], in_=cout[:, rt, :])
-            nc.scalar.activation(out=th[:, rt, :], in_=cout[:, rt, :], func=ACT.Tanh)
         chunk_w(2)
         chunk_q(1)
-        chunk_multiply(1)
-        chunk_sum(0)
-        sigmoid_one(last, 1, chunk_mm[1][:, 0, :])
         chunk_w(3)
         chunk_q(2)
-        chunk_multiply(2)
-        chunk_sum(1)
-        sigmoid_one(last, 2, chunk_mm[2][:, 0, :])
         chunk_q(3)
-        chunk_multiply(3)
-        chunk_sum(2)
-        sigmoid_one(last, 3, chunk_mm[3][:, 0, :])
-        chunk_out(0)
-        chunk_out(1)
-        chunk_sum(3)
-        chunk_out(2)
-        chunk_out(3)
+        for ft in all_ft:
+            chunk_multiply(ft)
+            sigmoid_one(last, ft, chunk_mm[ft][:, 0, :])
+        o_sum(last - 1, all_ft)
+        for ft in all_ft:
+            o_sum(last, [ft])
+            chunk_out(ft)

@@ -21,10 +21,11 @@ ROWS = 256
 NFT = 4
 ROUTED = 256
 RT = [1, 1, 1, 1, 1, 1, 1, 1, 1, 0, 0, 0]
-SH = [0, 0, 0, 0, 0, 0, 0, 0, 0, 128, 128, 0]
-NV = [1, 1, 1, 1, 1, 1, 0, 0, 0, 0, 0, 0]
+SH = [0, 0, 0, 0, 0, 0, 0, 0, 0, 128, 96, 0]
+NV = [1, 1, 1, 0, 1, 1, 0, 1, 0, 1, 0, 0]
 ZL = 0
 HS = 4
+GP = [0, 0, 0, 0, 0, 0, 0, 1, 1, 0, 0, 0]
 
 
 def tile_st_hmr_pb_kernel(tc, h_new, c_new, g_t, c_g_t, Wg_t, Zg_t_bytes, Zg_t_scale, bg_t, out_0, out_1):
@@ -45,7 +46,7 @@ def tile_st_hmr_pb_kernel(tc, h_new, c_new, g_t, c_g_t, Wg_t, Zg_t_bytes, Zg_t_s
         wpool = ctx.enter_context(tc.tile_pool(name="wpool", bufs=8))
         zpool = ctx.enter_context(tc.tile_pool(name="zpool", bufs=8))
         zwpool = ctx.enter_context(tc.tile_pool(name="zwpool", bufs=3 + ZL))
-        gpool = ctx.enter_context(tc.tile_pool(name="gpool", bufs=3))
+        gpool = ctx.enter_context(tc.tile_pool(name="gpool", bufs=2))
         qpool = ctx.enter_context(tc.tile_pool(name="qpool", bufs=4))
         spool = ctx.enter_context(tc.tile_pool(name="spool", bufs=2))
         psum_mm = ctx.enter_context(tc.psum_pool(name="psum_mm", bufs=4))
@@ -163,8 +164,16 @@ def tile_st_hmr_pb_kernel(tc, h_new, c_new, g_t, c_g_t, Wg_t, Zg_t_bytes, Zg_t_s
                     stop=True,
                 )
 
-        def interleave_scalar(u):
+        def pool_copy(out, in_):
+            nc.gpsimd.tensor_scalar(out=out, in0=in_, scalar1=1.0, scalar2=0.0, op0=ALU.mult, op1=ALU.add)
+
+        def interleave_pool(u):
             grouped[u] = gpool.tile([P, 2, H, 4], BF16, name="grouped", tag="grouped", align_bytes=64)
+            pool_copy(grouped[u][:, 0, ROUTED:H, :], wraw[u][:, :, ROUTED:H].rearrange("p j n -> p n j"))
+
+        def interleave_scalar(u):
+            if not GP[u]:
+                grouped[u] = gpool.tile([P, 2, H, 4], BF16, name="grouped", tag="grouped", align_bytes=64)
             lo = 0
             if RT[u]:
                 lo = ROUTED
@@ -175,6 +184,8 @@ def tile_st_hmr_pb_kernel(tc, h_new, c_new, g_t, c_g_t, Wg_t, Zg_t_bytes, Zg_t_s
                 )
 
         def interleave_w(u):
+            if GP[u]:
+                return
             lo = ROUTED * RT[u] + SH[u]
             nc.vector.tensor_copy(out=grouped[u][:, 0, lo:H, :], in_=wraw[u][:, :, lo:H].rearrange("p j n -> p n j"))
 
@@ -346,12 +357,17 @@ def tile_st_hmr_pb_kernel(tc, h_new, c_new, g_t, c_g_t, Wg_t, Zg_t_bytes, Zg_t_s
                         nc.tensor.transpose(out=xg[:, i2, u2, :], in_=words[:, u2::2], identity=ident_f[:])
                 bT = psum_tr.tile([P, P], BF16, name="bT", tag="tr")
                 nc.tensor.transpose(out=bT[:], in_=bias_raw[:], identity=ident_b[:])
+            if s < n_units and GP[s]:
+                interleave_pool(s)
             if s == 7:
                 times_c(0)
                 times_c(1)
             if s == 8:
                 times_c(2)
                 times_c(3)
+            if s == 11:
+                grp = gpool.tile([P, NFT, 2, P, 4], BF16, name="grp", tag="grouped", align_bytes=64)
+                pool_copy(grp[:, 2:4, 0, :, :], wraw[last][:, :, 2 * P : 4 * P].rearrange("p j (f n) -> p f n j", f=2))
             if s == 11:
                 for rt in range(2):
                     nc.vector.scalar_tensor_tensor(
@@ -380,7 +396,6 @@ def tile_st_hmr_pb_kernel(tc, h_new, c_new, g_t, c_g_t, Wg_t, Zg_t_bytes, Zg_t_s
             if c >= 0:
                 sigmoid(c)
 
-        grp = gpool.tile([P, NFT, 2, P, 4], BF16, name="grp", tag="grouped", align_bytes=64)
         codes[last] = qpool.tile([P, 2 * H], U32, name="codes_l", tag="codes", align_bytes=64)
         scales[last] = qpool.tile([P, 2 * H], U8, name="scales_l", tag="scales", align_bytes=64)
 
@@ -429,15 +444,13 @@ def tile_st_hmr_pb_kernel(tc, h_new, c_new, g_t, c_g_t, Wg_t, Zg_t_bytes, Zg_t_s
         chunk_w(1)
         chunk_z(1, nc.vector.tensor_copy)
         chunk_q(0)
-        chunk_w(2)
         chunk_q(1)
-        chunk_w(3)
         chunk_q(2)
         chunk_q(3)
         for ft in all_ft:
             chunk_multiply(ft)
             sigmoid_one(last, ft, chunk_mm[ft][:, 0, :])
-        o_sum(last - 1, all_ft)
         for ft in all_ft:
+            o_sum(last - 1, [ft])
             o_sum(last, [ft])
             chunk_out(ft)

@@ -164,6 +164,12 @@ def tile_st_hmr_pb_kernel(tc, h_new, c_new, g_t, c_g_t, Wg_t, Zg_t_bytes, Zg_t_s
                     stop=True,
                 )
 
+        def near_out(ap):
+            return ap.rearrange("p (c i) j -> p c j i", i=4)
+
+        def near_in(ap):
+            return ap.rearrange("p j (c i) -> p c j i", i=4)
+
         def pool_copy(out, in_):
             nc.gpsimd.tensor_scalar(out=out, in0=in_, scalar1=1.0, scalar2=0.0, op0=ALU.mult, op1=ALU.add)
 
@@ -179,18 +185,16 @@ def tile_st_hmr_pb_kernel(tc, h_new, c_new, g_t, c_g_t, Wg_t, Zg_t_bytes, Zg_t_s
                 lo = ROUTED
                 nc.scalar.copy(out=grouped[u][:, 0, 0:ROUTED, :].rearrange("p n j -> p (n j)"), in_=routed[u][:])
             if SH[u]:
-                nc.scalar.copy(
-                    out=grouped[u][:, 0, lo : lo + SH[u], :], in_=wraw[u][:, :, lo : lo + SH[u]].rearrange("p j n -> p n j")
-                )
+                nc.scalar.copy(out=near_out(grouped[u][:, 0, lo : lo + SH[u], :]), in_=near_in(wraw[u][:, :, lo : lo + SH[u]]))
 
         def interleave_w(u):
             if GP[u]:
                 return
             lo = ROUTED * RT[u] + SH[u]
-            nc.vector.tensor_copy(out=grouped[u][:, 0, lo:H, :], in_=wraw[u][:, :, lo:H].rearrange("p j n -> p n j"))
+            nc.vector.tensor_copy(out=near_out(grouped[u][:, 0, lo:H, :]), in_=near_in(wraw[u][:, :, lo:H]))
 
         def interleave_z(u):
-            nc.vector.tensor_copy(out=grouped[u][:, 1, :, :], in_=zwide[u][:].rearrange("p j n -> p n j"))
+            nc.vector.tensor_copy(out=near_out(grouped[u][:, 1, :, :]), in_=near_in(zwide[u][:]))
 
         def quantize(u):
             codes[u] = qpool.tile([P, 2 * H], U32, name="codes", tag="codes", align_bytes=64)
@@ -400,12 +404,10 @@ def tile_st_hmr_pb_kernel(tc, h_new, c_new, g_t, c_g_t, Wg_t, Zg_t_bytes, Zg_t_s
         scales[last] = qpool.tile([P, 2 * H], U8, name="scales_l", tag="scales", align_bytes=64)
 
         def chunk_w(ft):
-            nc.vector.tensor_copy(
-                out=grp[:, ft, 0, :, :], in_=wraw[last][:, :, ft * P : (ft + 1) * P].rearrange("p j n -> p n j")
-            )
+            nc.vector.tensor_copy(out=near_out(grp[:, ft, 0, :, :]), in_=near_in(wraw[last][:, :, ft * P : (ft + 1) * P]))
 
         def chunk_z(ft, engine_copy):
-            engine_copy(out=grp[:, ft, 1, :, :], in_=zwide[last][:, :, ft * P : (ft + 1) * P].rearrange("p j n -> p n j"))
+            engine_copy(out=near_out(grp[:, ft, 1, :, :]), in_=near_in(zwide[last][:, :, ft * P : (ft + 1) * P]))
 
         def chunk_q(ft):
             nc.vector.quantize_mx(

@@ -20,8 +20,8 @@ T = 4
 ROWS = 256
 NFT = 4
 ROUTED = 256
-RT = [1, 1, 1, 1, 1, 1, 1, 1, 1, 0, 0, 0]
-SH = [0, 0, 0, 0, 0, 0, 0, 0, 0, 128, 96, 0]
+RT = [1, 1, 1, 1, 1, 1, 1, 0, 0, 1, 1, 0]
+SH = [0, 0, 0, 0, 0, 0, 0, 128, 96, 0, 0, 0]
 NV = [1, 1, 1, 0, 1, 1, 0, 1, 0, 1, 0, 0]
 ZL = 0
 HS = 4
@@ -154,7 +154,10 @@ def tile_st_hmr_pb_kernel(tc, h_new, c_new, g_t, c_g_t, Wg_t, Zg_t_bytes, Zg_t_s
                     nc.scalar.activation(out=zwide[u][:, j, :], in_=src, func=ACT.Copy, scale=zs[:, j : j + 1])
 
         def route(u):
-            routed[u] = psum_acc.tile([P, 4 * ROUTED], BF16, name="routed", tag="acc")
+            if u < 9:
+                routed[u] = psum_acc.tile([P, 4 * ROUTED], BF16, name="routed", tag="acc")
+            else:
+                routed[u] = psum_tr.tile([P, 4 * ROUTED], BF16, name="routed_t", tag="tr")
             for half in range(2):
                 nc.tensor.matmul(
                     out=routed[u][:].rearrange("p (n k e) -> p k n e", k=2, e=2)[:, half, :, :],
@@ -188,10 +191,10 @@ def tile_st_hmr_pb_kernel(tc, h_new, c_new, g_t, c_g_t, Wg_t, Zg_t_bytes, Zg_t_s
                 nc.scalar.copy(out=near_out(grouped[u][:, 0, lo : lo + SH[u], :]), in_=near_in(wraw[u][:, :, lo : lo + SH[u]]))
 
         def interleave_w(u):
-            if GP[u]:
-                return
             lo = ROUTED * RT[u] + SH[u]
-            nc.vector.tensor_copy(out=near_out(grouped[u][:, 0, lo:H, :]), in_=near_in(wraw[u][:, :, lo:H]))
+            hi = ROUTED if GP[u] else H
+            if lo < hi:
+                nc.vector.tensor_copy(out=near_out(grouped[u][:, 0, lo:hi, :]), in_=near_in(wraw[u][:, :, lo:hi]))
 
         def interleave_z(u):
             nc.vector.tensor_copy(out=near_out(grouped[u][:, 1, :, :]), in_=near_in(zwide[u][:]))
@@ -330,7 +333,8 @@ def tile_st_hmr_pb_kernel(tc, h_new, c_new, g_t, c_g_t, Wg_t, Zg_t_bytes, Zg_t_s
             if s == 11:
                 g_acc = sum_frames(1, psum_tr, "tr")
             if a >= 0:
-                interleave_scalar(a)
+                if a != 10:
+                    interleave_scalar(a)
                 interleave_w(a)
             if s == 1:
                 for q in range(4):
@@ -395,10 +399,16 @@ def tile_st_hmr_pb_kernel(tc, h_new, c_new, g_t, c_g_t, Wg_t, Zg_t_bytes, Zg_t_s
             if s == 7:
                 turn_c(2)
                 turn_c(3)
-            if s == 9:
-                f_acc = sum_frames(0, psum_acc, "acc")
+            if s == 8:
+                f_acc = [psum_acc.tile([P, H], F32, name="acc_acc", tag="acc") for rt in range(2)]
+            if s == 8 or s == 9:
+                for rt in range(2):
+                    for ft in (2 * (s - 8), 2 * (s - 8) + 1):
+                        sum_group(f_acc[rt][:, ft * P : (ft + 1) * P], 0, ft, rt)
             if c >= 0:
                 sigmoid(c)
+            if s == 10:
+                interleave_scalar(10)
 
         codes[last] = qpool.tile([P, 2 * H], U32, name="codes_l", tag="codes", align_bytes=64)
         scales[last] = qpool.tile([P, 2 * H], U8, name="scales_l", tag="scales", align_bytes=64)

@@ -22,10 +22,11 @@ NFT = 4
 ROUTED = 256
 RT = [1, 1, 1, 1, 1, 1, 1, 0, 0, 1, 1, 0]
 SH = [0, 0, 0, 0, 0, 0, 0, 128, 96, 0, 0, 0]
-NV = [1, 1, 1, 0, 1, 1, 0, 1, 0, 1, 0, 0]
+NV = [2, 1, 1, 0, 1, 1, 0, 1, 0, 1, 0, 0]
 ZL = 0
 HS = 4
 GP = [0, 0, 0, 0, 0, 0, 0, 1, 1, 0, 0, 0]
+GZ = [0, 0, 0, 0, 0, 0, 96, 96, 0, 0, 96, 0]
 
 
 def tile_st_hmr_pb_kernel(tc, h_new, c_new, g_t, c_g_t, Wg_t, Zg_t_bytes, Zg_t_scale, bg_t, out_0, out_1):
@@ -180,9 +181,11 @@ def tile_st_hmr_pb_kernel(tc, h_new, c_new, g_t, c_g_t, Wg_t, Zg_t_bytes, Zg_t_s
             grouped[u] = gpool.tile([P, 2, H, 4], BF16, name="grouped", tag="grouped", align_bytes=64)
             pool_copy(grouped[u][:, 0, ROUTED:H, :], wraw[u][:, :, ROUTED:H].rearrange("p j n -> p n j"))
 
-        def interleave_scalar(u):
+        def alloc_grouped(u):
             if not GP[u]:
                 grouped[u] = gpool.tile([P, 2, H, 4], BF16, name="grouped", tag="grouped", align_bytes=64)
+
+        def interleave_scalar(u):
             lo = 0
             if RT[u]:
                 lo = ROUTED
@@ -197,7 +200,10 @@ def tile_st_hmr_pb_kernel(tc, h_new, c_new, g_t, c_g_t, Wg_t, Zg_t_bytes, Zg_t_s
                 nc.vector.tensor_copy(out=near_out(grouped[u][:, 0, lo:hi, :]), in_=near_in(wraw[u][:, :, lo:hi]))
 
         def interleave_z(u):
-            nc.vector.tensor_copy(out=near_out(grouped[u][:, 1, :, :]), in_=near_in(zwide[u][:]))
+            nc.vector.tensor_copy(out=near_out(grouped[u][:, 1, 0 : H - GZ[u], :]), in_=near_in(zwide[u][:, :, 0 : H - GZ[u]]))
+
+        def interleave_z_pool(u):
+            pool_copy(grouped[u][:, 1, H - GZ[u] : H, :], zwide[u][:, :, H - GZ[u] : H].rearrange("p j n -> p n j"))
 
         def quantize(u):
             codes[u] = qpool.tile([P, 2 * H], U32, name="codes", tag="codes", align_bytes=64)
@@ -334,6 +340,8 @@ def tile_st_hmr_pb_kernel(tc, h_new, c_new, g_t, c_g_t, Wg_t, Zg_t_bytes, Zg_t_s
                 g_acc = sum_frames(1, psum_tr, "tr")
             if a >= 0:
                 if a != 10:
+                    alloc_grouped(a)
+                if a != 10 and a != 0:
                     interleave_scalar(a)
                 interleave_w(a)
             if s == 1:
@@ -367,6 +375,7 @@ def tile_st_hmr_pb_kernel(tc, h_new, c_new, g_t, c_g_t, Wg_t, Zg_t_bytes, Zg_t_s
                 nc.tensor.transpose(out=bT[:], in_=bias_raw[:], identity=ident_b[:])
             if s < n_units and GP[s]:
                 interleave_pool(s)
+                interleave_z_pool(a)
             if s == 7:
                 times_c(0)
                 times_c(1)
@@ -376,6 +385,7 @@ def tile_st_hmr_pb_kernel(tc, h_new, c_new, g_t, c_g_t, Wg_t, Zg_t_bytes, Zg_t_s
             if s == 11:
                 grp = gpool.tile([P, NFT, 2, P, 4], BF16, name="grp", tag="grouped", align_bytes=64)
                 pool_copy(grp[:, 2:4, 0, :, :], wraw[last][:, :, 2 * P : 4 * P].rearrange("p j (f n) -> p f n j", f=2))
+                interleave_z_pool(a)
             if s == 11:
                 for rt in range(2):
                     nc.vector.scalar_tensor_tensor(
@@ -388,6 +398,8 @@ def tile_st_hmr_pb_kernel(tc, h_new, c_new, g_t, c_g_t, Wg_t, Zg_t_bytes, Zg_t_s
                     nc.sync.dma_start(out=out1_rows[:, rt, :], in_=cout[:, rt, :])
             if w < n_units:
                 widen(w, NV[w])
+            if s == 1:
+                interleave_scalar(0)
             if s == 3:
                 nc.scalar.copy(out=bias_sb[:], in_=bT[:, 0:48])
                 multiply(0)
@@ -408,6 +420,7 @@ def tile_st_hmr_pb_kernel(tc, h_new, c_new, g_t, c_g_t, Wg_t, Zg_t_bytes, Zg_t_s
             if c >= 0:
                 sigmoid(c)
             if s == 10:
+                alloc_grouped(10)
                 interleave_scalar(10)
 
         codes[last] = qpool.tile([P, 2 * H], U32, name="codes_l", tag="codes", align_bytes=64)

@@ -26,7 +26,7 @@ NV = [2, 1, 1, 0, 1, 1, 0, 1, 0, 1, 0, 0]
 ZL = 0
 HS = 4
 GP = [0, 0, 0, 0, 0, 0, 0, 1, 1, 0, 0, 0]
-GZ = [0, 0, 0, 0, 0, 0, 96, 96, 0, 0, 96, 0]
+GZ = [0, 0, 0, 0, 0, 0, 96, 96, 0, 0, 0, 0]
 
 
 def tile_st_hmr_pb_kernel(tc, h_new, c_new, g_t, c_g_t, Wg_t, Zg_t_bytes, Zg_t_scale, bg_t, out_0, out_1):
@@ -382,20 +382,6 @@ def tile_st_hmr_pb_kernel(tc, h_new, c_new, g_t, c_g_t, Wg_t, Zg_t_bytes, Zg_t_s
             if s == 8:
                 times_c(2)
                 times_c(3)
-            if s == 11:
-                grp = gpool.tile([P, NFT, 2, P, 4], BF16, name="grp", tag="grouped", align_bytes=64)
-                pool_copy(grp[:, 2:4, 0, :, :], wraw[last][:, :, 2 * P : 4 * P].rearrange("p j (f n) -> p f n j", f=2))
-                interleave_z_pool(a)
-            if s == 11:
-                for rt in range(2):
-                    nc.vector.scalar_tensor_tensor(
-                        out=tmp[:, rt, :], in0=g_acc[rt][:], scalar=0.25, in1=cg_sb[:, rt, :], op0=ALU.mult, op1=ALU.mult
-                    )
-                for rt in range(2):
-                    nc.vector.scalar_tensor_tensor(
-                        out=cout[:, rt, :], in0=f_acc[rt][:], scalar=0.25, in1=tmp[:, rt, :], op0=ALU.mult, op1=ALU.add
-                    )
-                    nc.sync.dma_start(out=out1_rows[:, rt, :], in_=cout[:, rt, :])
             if w < n_units:
                 widen(w, NV[w])
             if s == 1:
@@ -426,17 +412,22 @@ def tile_st_hmr_pb_kernel(tc, h_new, c_new, g_t, c_g_t, Wg_t, Zg_t_bytes, Zg_t_s
         codes[last] = qpool.tile([P, 2 * H], U32, name="codes_l", tag="codes", align_bytes=64)
         scales[last] = qpool.tile([P, 2 * H], U8, name="scales_l", tag="scales", align_bytes=64)
 
+        halves = {}
+
+        def chunk_tile(ft):
+            return halves[ft // 2][:, ft % 2, :, :, :]
+
         def chunk_w(ft):
-            nc.vector.tensor_copy(out=near_out(grp[:, ft, 0, :, :]), in_=near_in(wraw[last][:, :, ft * P : (ft + 1) * P]))
+            nc.vector.tensor_copy(out=near_out(chunk_tile(ft)[:, 0, :, :]), in_=near_in(wraw[last][:, :, ft * P : (ft + 1) * P]))
 
         def chunk_z(ft, engine_copy):
-            engine_copy(out=near_out(grp[:, ft, 1, :, :]), in_=near_in(zwide[last][:, :, ft * P : (ft + 1) * P]))
+            engine_copy(out=near_out(chunk_tile(ft)[:, 1, :, :]), in_=near_in(zwide[last][:, :, ft * P : (ft + 1) * P]))
 
         def chunk_q(ft):
             nc.vector.quantize_mx(
                 out=codes[last][:, ft * 2 * P : (ft + 1) * 2 * P].bitcast(FP8X4),
                 scales=scales[last][:, ft * 2 * P : (ft + 1) * 2 * P],
-                in_=grp[:, ft, :, :, :].rearrange("p a n j -> p (a n j)"),
+                in_=chunk_tile(ft).rearrange("p a n j -> p (a n j)"),
             )
 
         chunk_mm = {}
@@ -454,17 +445,29 @@ def tile_st_hmr_pb_kernel(tc, h_new, c_new, g_t, c_g_t, Wg_t, Zg_t_bytes, Zg_t_s
             nc.sync.dma_start(out=out0_rows[:, :, cols], in_=gout[:, :, cols])
 
         all_ft = range(NFT)
-        chunk_z(2, nc.scalar.copy)
-        chunk_z(3, nc.scalar.copy)
+        halves[0] = gpool.tile([P, 2, 2, P, 4], BF16, name="half_a", tag="grouped", align_bytes=64)
+        chunk_w(0)
         sigmoid(last - 2)
-        o_sum(last - 3, all_ft)
         quantize(last - 1)
         multiply(last - 1)
+        halves[1] = gpool.tile([P, 2, 2, P, 4], BF16, name="half_b", tag="grouped", align_bytes=64)
+        pool_copy(halves[1][:, :, 0, :, :], wraw[last][:, :, 2 * P : 4 * P].rearrange("p j (f n) -> p f n j", f=2))
+        for rt in range(2):
+            nc.vector.scalar_tensor_tensor(
+                out=tmp[:, rt, :], in0=g_acc[rt][:], scalar=0.25, in1=cg_sb[:, rt, :], op0=ALU.mult, op1=ALU.mult
+            )
+        for rt in range(2):
+            nc.vector.scalar_tensor_tensor(
+                out=cout[:, rt, :], in0=f_acc[rt][:], scalar=0.25, in1=tmp[:, rt, :], op0=ALU.mult, op1=ALU.add
+            )
+            nc.sync.dma_start(out=out1_rows[:, rt, :], in_=cout[:, rt, :])
+        o_sum(last - 3, all_ft)
         o_sum(last - 2, all_ft)
+        chunk_z(2, nc.scalar.copy)
+        chunk_z(3, nc.scalar.copy)
         for rt in range(2):
             nc.scalar.activation(out=th[:, rt, :], in_=cout[:, rt, :], func=ACT.Tanh)
         sigmoid(last - 1)
-        chunk_w(0)
         chunk_z(0, nc.vector.tensor_copy)
         chunk_w(1)
         chunk_z(1, nc.vector.tensor_copy)

@@ -20,8 +20,8 @@ T = 4
 ROWS = 256
 NFT = 4
 ROUTED = 256
-RT = [1, 1, 1, 1, 1, 1, 1, 0, 0, 1, 1, 0]
-SH = [0, 0, 0, 0, 0, 0, 0, 128, 96, 0, 0, 0]
+RT = [256, 256, 256, 256, 256, 256, 256, 128, 0, 256, 256, 0]
+SH = [0, 0, 0, 0, 0, 0, 0, 0, 96, 0, 0, 0]
 NV = [2, 1, 1, 0, 1, 1, 0, 1, 0, 1, 0, 0]
 ZL = 0
 HS = 4
@@ -93,33 +93,47 @@ def tile_st_hmr_pb_kernel(tc, h_new, c_new, g_t, c_g_t, Wg_t, Zg_t_bytes, Zg_t_s
             wraw[u] = wpool.tile([P, 4, H], BF16, name="wraw", tag="wraw")
             nc.sync.dma_start(out=wraw[u][:], in_=Wg_t[g, t].rearrange("(p j) n -> p j n", j=4))
 
+        h_sb = [const.tile([P, 2, H], BF16, name="h_sb%d" % q) for q in range(4)]
+        g_sb = const.tile([P, 2, H], BF16, name="g_sb")
+        c_sb = const.tile([P, 8, H], BF16, name="c_sb")
+        cg_sb = const.tile([P, 2, H], BF16, name="cg_sb")
+
+        def load_h(q):
+            nc.sync.dma_start(out=h_sb[q][:], in_=h_rows[:, 2 * q : 2 * q + 2, :])
+
         load_z(0)
         load_w(0)
         load_z(1)
         load_w(1)
-        h_sb = []
-        for q in range(4):
-            hq = const.tile([P, 2, H], BF16, name="h_sb%d" % q)
-            nc.sync.dma_start(out=hq[:], in_=h_rows[:, 2 * q : 2 * q + 2, :])
-            h_sb.append(hq)
+        load_h(0)
+        load_h(1)
+        load_h(2)
+        load_h(3)
         load_z(2)
         load_w(2)
-        g_sb = const.tile([P, 2, H], BF16, name="g_sb")
         nc.sync.dma_start(out=g_sb[:], in_=g_rows)
         nc.sync.dma_start(out=bias_raw[0:48, :], in_=bg_t.rearrange("g t o (c f) -> (g t o c) f", f=P))
         load_z(3)
         load_w(3)
-        c_sb = const.tile([P, 8, H], BF16, name="c_sb")
         nc.sync.dma_start(out=c_sb[:, 0:4, :], in_=c_rows[:, 0:4, :])
         nc.sync.dma_start(out=c_sb[:, 4:8, :], in_=c_rows[:, 4:8, :])
-        for u in range(4, 7):
-            load_z(u)
-            load_w(u)
-        cg_sb = const.tile([P, 2, H], BF16, name="cg_sb")
+        load_z(4)
+        load_w(4)
+        load_z(5)
+        load_w(5)
+        load_z(6)
+        load_w(6)
         nc.sync.dma_start(out=cg_sb[:], in_=cg_rows)
-        for u in range(7, n_units):
-            load_z(u)
-            load_w(u)
+        load_z(7)
+        load_w(7)
+        load_z(8)
+        load_w(8)
+        load_z(9)
+        load_w(9)
+        load_z(10)
+        load_w(10)
+        load_z(11)
+        load_w(11)
 
         hg = const.tile([P, T, ROWS, 4], BF16, name="hg", align_bytes=64)
         hg32 = hg[:].rearrange("p t r e -> p (t r e)").bitcast(F32).rearrange("p (t r u) -> p t r u", t=T, u=2)
@@ -156,14 +170,14 @@ def tile_st_hmr_pb_kernel(tc, h_new, c_new, g_t, c_g_t, Wg_t, Zg_t_bytes, Zg_t_s
 
         def route(u):
             if u < 9:
-                routed[u] = psum_acc.tile([P, 4 * ROUTED], BF16, name="routed", tag="acc")
+                routed[u] = psum_acc.tile([P, 4 * RT[u]], BF16, name="routed", tag="acc")
             else:
-                routed[u] = psum_tr.tile([P, 4 * ROUTED], BF16, name="routed_t", tag="tr")
+                routed[u] = psum_tr.tile([P, 4 * RT[u]], BF16, name="routed_t", tag="tr")
             for half in range(2):
                 nc.tensor.matmul(
                     out=routed[u][:].rearrange("p (n k e) -> p k n e", k=2, e=2)[:, half, :, :],
                     lhsT=ident_b[:],
-                    rhs=wraw[u][:, 2 * half : 2 * half + 2, 0:ROUTED].rearrange("p e n -> p n e"),
+                    rhs=wraw[u][:, 2 * half : 2 * half + 2, 0 : RT[u]].rearrange("p e n -> p n e"),
                     start=True,
                     stop=True,
                 )
@@ -186,15 +200,14 @@ def tile_st_hmr_pb_kernel(tc, h_new, c_new, g_t, c_g_t, Wg_t, Zg_t_bytes, Zg_t_s
                 grouped[u] = gpool.tile([P, 2, H, 4], BF16, name="grouped", tag="grouped", align_bytes=64)
 
         def interleave_scalar(u):
-            lo = 0
+            lo = RT[u]
             if RT[u]:
-                lo = ROUTED
-                nc.scalar.copy(out=grouped[u][:, 0, 0:ROUTED, :].rearrange("p n j -> p (n j)"), in_=routed[u][:])
+                nc.scalar.copy(out=grouped[u][:, 0, 0 : RT[u], :].rearrange("p n j -> p (n j)"), in_=routed[u][:])
             if SH[u]:
                 nc.scalar.copy(out=near_out(grouped[u][:, 0, lo : lo + SH[u], :]), in_=near_in(wraw[u][:, :, lo : lo + SH[u]]))
 
         def interleave_w(u):
-            lo = ROUTED * RT[u] + SH[u]
+            lo = RT[u] + SH[u]
             hi = ROUTED if GP[u] else H
             if lo < hi:
                 nc.vector.tensor_copy(out=near_out(grouped[u][:, 0, lo:hi, :]), in_=near_in(wraw[u][:, :, lo:hi]))
@@ -452,6 +465,7 @@ def tile_st_hmr_pb_kernel(tc, h_new, c_new, g_t, c_g_t, Wg_t, Zg_t_bytes, Zg_t_s
         multiply(last - 1)
         halves[1] = gpool.tile([P, 2, 2, P, 4], BF16, name="half_b", tag="grouped", align_bytes=64)
         pool_copy(halves[1][:, :, 0, :, :], wraw[last][:, :, 2 * P : 4 * P].rearrange("p j (f n) -> p f n j", f=2))
+        pool_copy(chunk_tile(3)[:, 1, :, :], zwide[last][:, :, 3 * P : 4 * P].rearrange("p j n -> p n j"))
         for rt in range(2):
             nc.vector.scalar_tensor_tensor(
                 out=tmp[:, rt, :], in0=g_acc[rt][:], scalar=0.25, in1=cg_sb[:, rt, :], op0=ALU.mult, op1=ALU.mult
@@ -464,7 +478,6 @@ def tile_st_hmr_pb_kernel(tc, h_new, c_new, g_t, c_g_t, Wg_t, Zg_t_bytes, Zg_t_s
         o_sum(last - 3, all_ft)
         o_sum(last - 2, all_ft)
         chunk_z(2, nc.scalar.copy)
-        chunk_z(3, nc.scalar.copy)
         for rt in range(2):
             nc.scalar.activation(out=th[:, rt, :], in_=cout[:, rt, :], func=ACT.Tanh)
         sigmoid(last - 1)

@@ -22,9 +22,7 @@ NFT = 4
 ROUTED = 256
 RT = [256, 256, 256, 256, 256, 256, 256, 128, 0, 256, 256, 0]
 SH = [0, 0, 0, 0, 0, 0, 0, 0, 96, 0, 0, 0]
-NV = [2, 1, 1, 0, 1, 1, 0, 1, 0, 1, 0, 0]
-ZL = 0
-HS = 4
+NV = [3,0,1,0,1,1,1,1,0,1,0,0]
 GP = [0, 0, 0, 0, 0, 0, 0, 1, 1, 0, 0, 0]
 GZ = [0, 0, 0, 0, 0, 0, 96, 96, 0, 0, 0, 0]
 
@@ -46,7 +44,7 @@ def tile_st_hmr_pb_kernel(tc, h_new, c_new, g_t, c_g_t, Wg_t, Zg_t_bytes, Zg_t_s
         const = ctx.enter_context(tc.tile_pool(name="const", bufs=1))
         wpool = ctx.enter_context(tc.tile_pool(name="wpool", bufs=8))
         zpool = ctx.enter_context(tc.tile_pool(name="zpool", bufs=8))
-        zwpool = ctx.enter_context(tc.tile_pool(name="zwpool", bufs=3 + ZL))
+        zwpool = ctx.enter_context(tc.tile_pool(name="zwpool", bufs=3))
         gpool = ctx.enter_context(tc.tile_pool(name="gpool", bufs=2))
         qpool = ctx.enter_context(tc.tile_pool(name="qpool", bufs=4))
         spool = ctx.enter_context(tc.tile_pool(name="spool", bufs=2))
@@ -102,23 +100,23 @@ def tile_st_hmr_pb_kernel(tc, h_new, c_new, g_t, c_g_t, Wg_t, Zg_t_bytes, Zg_t_s
             nc.sync.dma_start(out=h_sb[q][:], in_=h_rows[:, 2 * q : 2 * q + 2, :])
 
         load_z(0)
-        load_w(0)
         load_z(1)
+        load_w(0)
         load_w(1)
+        load_z(2)
         load_h(0)
         load_h(1)
+        load_w(2)
+        load_z(3)
         load_h(2)
         load_h(3)
-        load_z(2)
-        load_w(2)
+        load_w(3)
         nc.sync.dma_start(out=g_sb[:], in_=g_rows)
         nc.sync.dma_start(out=bias_raw[0:48, :], in_=bg_t.rearrange("g t o (c f) -> (g t o c) f", f=P))
-        load_z(3)
-        load_w(3)
-        nc.sync.dma_start(out=c_sb[:, 0:4, :], in_=c_rows[:, 0:4, :])
-        nc.sync.dma_start(out=c_sb[:, 4:8, :], in_=c_rows[:, 4:8, :])
         load_z(4)
         load_w(4)
+        nc.sync.dma_start(out=c_sb[:, 0:4, :], in_=c_rows[:, 0:4, :])
+        nc.sync.dma_start(out=c_sb[:, 4:8, :], in_=c_rows[:, 4:8, :])
         load_z(5)
         load_w(5)
         load_z(6)
@@ -248,14 +246,16 @@ def tile_st_hmr_pb_kernel(tc, h_new, c_new, g_t, c_g_t, Wg_t, Zg_t_bytes, Zg_t_s
                 stop=True,
             )
 
+        def multiply_part(u, fts):
+            for ft in fts:
+                if ft == 0:
+                    banks[u] = []
+                if ft % 2 == 0:
+                    banks[u].append(psum_mm.tile([P, 2, ROWS], F32, name="mm", tag="mm"))
+                gate_pair(banks[u][ft // 2][:, ft % 2, :], u, slice(ft * P, (ft + 1) * P), slice(H + ft * P, H + (ft + 1) * P))
+
         def multiply(u):
-            banks[u] = []
-            for b in range(2):
-                mm = psum_mm.tile([P, 2, ROWS], F32, name="mm", tag="mm")
-                for f2 in range(2):
-                    ft = 2 * b + f2
-                    gate_pair(mm[:, f2, :], u, slice(ft * P, (ft + 1) * P), slice(H + ft * P, H + (ft + 1) * P))
-                banks[u].append(mm)
+            multiply_part(u, range(NFT))
 
         def sigmoid_one(u, ft, src):
             g, t = units[u]
@@ -339,46 +339,39 @@ def tile_st_hmr_pb_kernel(tc, h_new, c_new, g_t, c_g_t, Wg_t, Zg_t_bytes, Zg_t_s
                         stop=(t == T - 1 and rt == 1),
                     )
 
-        for z in range(ZL):
-            widen(z, NV[z])
-
+        EARLY = [4, 10]
         for s in range(n_units):
             a = s - 1
             b = s - 2
             c = s - 3
-            w = s + ZL
             if RT[s]:
                 route(s)
             if s == 11:
                 g_acc = sum_frames(1, psum_tr, "tr")
-            if a >= 0:
-                if a != 10:
-                    alloc_grouped(a)
-                if a != 10 and a != 0:
+            if a >= 0 and a not in EARLY:
+                alloc_grouped(a)
+                if a != 0:
                     interleave_scalar(a)
+            if a == 0:
+                interleave_z(a)
+            if a >= 0:
                 interleave_w(a)
-            if s == 1:
-                for q in range(4):
-                    turn_h(q)
-            if s == 2:
-                for q in range(HS):
-                    h_out(q, nc.scalar.copy)
-            if s == 3:
+            if s == 1 or s == 2:
+                turn_h(2 * s - 2)
+                turn_h(2 * s - 1)
+            if b >= 0:
+                quantize(b)
+            if s == 4:
+                nc.vector.tensor_copy(out=gg32, in_=xg[:].rearrange("p i u r -> p i r u"))
                 nc.vector.quantize_mx(
                     out=h_codes[:].bitcast(FP8X4), scales=h_scales[:], in_=hg[:].rearrange("p t r e -> p (t r e)")
                 )
-                nc.vector.tensor_copy(out=gg32, in_=xg[:].rearrange("p i u r -> p i r u"))
-            if b >= 0:
-                quantize(b)
-            if s == 3:
                 nc.vector.quantize_mx(
                     out=g_codes[:].bitcast(FP8X4), scales=g_scales[:], in_=gg[:].rearrange("p r e -> p (r e)")
                 )
-            if a >= 0:
+            if a >= 1:
                 interleave_z(a)
-            if s == 2:
-                for q in range(HS, 4):
-                    h_out(q, nc.vector.tensor_copy)
+            if s == 3:
                 xg = psum_mm.tile([P, 2, 2, P], F32, name="xg", tag="mm")
                 for i2 in range(2):
                     words = g_sb[:, i2, :].bitcast(F32)
@@ -386,7 +379,7 @@ def tile_st_hmr_pb_kernel(tc, h_new, c_new, g_t, c_g_t, Wg_t, Zg_t_bytes, Zg_t_s
                         nc.tensor.transpose(out=xg[:, i2, u2, :], in_=words[:, u2::2], identity=ident_f[:])
                 bT = psum_tr.tile([P, P], BF16, name="bT", tag="tr")
                 nc.tensor.transpose(out=bT[:], in_=bias_raw[:], identity=ident_b[:])
-            if s < n_units and GP[s]:
+            if GP[s]:
                 interleave_pool(s)
                 interleave_z_pool(a)
             if s == 7:
@@ -395,14 +388,17 @@ def tile_st_hmr_pb_kernel(tc, h_new, c_new, g_t, c_g_t, Wg_t, Zg_t_bytes, Zg_t_s
             if s == 8:
                 times_c(2)
                 times_c(3)
-            if w < n_units:
-                widen(w, NV[w])
+            widen(s, NV[s])
             if s == 1:
                 interleave_scalar(0)
-            if s == 3:
+            if s == 2 or s == 3:
+                h_out(2 * s - 4, nc.scalar.copy)
+                h_out(2 * s - 3, nc.scalar.copy)
+            if s == 4:
                 nc.scalar.copy(out=bias_sb[:], in_=bT[:, 0:48])
                 multiply(0)
-            if b >= 1:
+                multiply(1)
+            if b >= 2:
                 multiply(b)
             if s == 5:
                 turn_c(0)
@@ -416,7 +412,11 @@ def tile_st_hmr_pb_kernel(tc, h_new, c_new, g_t, c_g_t, Wg_t, Zg_t_bytes, Zg_t_s
                 for rt in range(2):
                     for ft in (2 * (s - 8), 2 * (s - 8) + 1):
                         sum_group(f_acc[rt][:, ft * P : (ft + 1) * P], 0, ft, rt)
-            if c >= 0:
+            if s == 4:
+                alloc_grouped(4)
+                interleave_scalar(4)
+                sigmoid(0)
+            if c >= 1:
                 sigmoid(c)
             if s == 10:
                 alloc_grouped(10)
@@ -460,7 +460,6 @@ def tile_st_hmr_pb_kernel(tc, h_new, c_new, g_t, c_g_t, Wg_t, Zg_t_bytes, Zg_t_s
         all_ft = range(NFT)
         halves[0] = gpool.tile([P, 2, 2, P, 4], BF16, name="half_a", tag="grouped", align_bytes=64)
         chunk_w(0)
-        sigmoid(last - 2)
         quantize(last - 1)
         multiply(last - 1)
         halves[1] = gpool.tile([P, 2, 2, P, 4], BF16, name="half_b", tag="grouped", align_bytes=64)
@@ -476,10 +475,11 @@ def tile_st_hmr_pb_kernel(tc, h_new, c_new, g_t, c_g_t, Wg_t, Zg_t_bytes, Zg_t_s
             )
             nc.sync.dma_start(out=out1_rows[:, rt, :], in_=cout[:, rt, :])
         o_sum(last - 3, all_ft)
-        o_sum(last - 2, all_ft)
         chunk_z(2, nc.scalar.copy)
+        sigmoid(last - 2)
         for rt in range(2):
             nc.scalar.activation(out=th[:, rt, :], in_=cout[:, rt, :], func=ACT.Tanh)
+        o_sum(last - 2, all_ft)
         sigmoid(last - 1)
         chunk_z(0, nc.vector.tensor_copy)
         chunk_w(1)

@@ -350,7 +350,7 @@ def tile_st_hmr_pb_kernel(tc, h_new, c_new, g_t, c_g_t, Wg_t, Zg_t_bytes, Zg_t_s
                 g_acc = sum_frames(1, psum_tr, "tr")
             if a >= 0 and a not in EARLY:
                 alloc_grouped(a)
-                if a != 0:
+                if a > 1:
                     interleave_scalar(a)
             if a == 0:
                 interleave_z(a)
@@ -389,8 +389,8 @@ def tile_st_hmr_pb_kernel(tc, h_new, c_new, g_t, c_g_t, Wg_t, Zg_t_bytes, Zg_t_s
                 times_c(2)
                 times_c(3)
             widen(s, NV[s])
-            if s == 1:
-                interleave_scalar(0)
+            if s == 1 or s == 2:
+                interleave_scalar(a)
             if s == 2 or s == 3:
                 h_out(2 * s - 4, nc.scalar.copy)
                 h_out(2 * s - 3, nc.scalar.copy)
@@ -477,10 +477,11 @@ def tile_st_hmr_pb_kernel(tc, h_new, c_new, g_t, c_g_t, Wg_t, Zg_t_bytes, Zg_t_s
         o_sum(last - 3, all_ft)
         chunk_z(2, nc.scalar.copy)
         sigmoid(last - 2)
-        for rt in range(2):
-            nc.scalar.activation(out=th[:, rt, :], in_=cout[:, rt, :], func=ACT.Tanh)
         o_sum(last - 2, all_ft)
         sigmoid(last - 1)
+        for rt in range(2):
+            nc.scalar.activation(out=th[:, rt, :], in_=cout[:, rt, :], func=ACT.Tanh)
+        o_sum(last - 1, (0, 1,))
         chunk_z(0, nc.vector.tensor_copy)
         chunk_w(1)
         chunk_z(1, nc.vector.tensor_copy)
@@ -492,6 +493,7 @@ def tile_st_hmr_pb_kernel(tc, h_new, c_new, g_t, c_g_t, Wg_t, Zg_t_bytes, Zg_t_s
             chunk_multiply(ft)
             sigmoid_one(last, ft, chunk_mm[ft][:, 0, :])
         for ft in all_ft:
-            o_sum(last - 1, [ft])
+            if ft not in (0, 1,):
+                o_sum(last - 1, [ft])
             o_sum(last, [ft])
             chunk_out(ft)

@@ -24,7 +24,7 @@ RT = [256, 256, 256, 256, 256, 256, 256, 128, 0, 256, 256, 0]
 SH = [0, 0, 0, 0, 0, 0, 0, 0, 96, 0, 0, 0]
 NV = [3,0,1,0,1,1,1,1,0,1,0,0]
 GP = [0, 0, 0, 0, 0, 0, 0, 1, 1, 0, 0, 0]
-GZ = [0, 0, 0, 0, 0, 0, 96, 96, 0, 0, 0, 0]
+GZ = [0, 0, 0, 0, 0, 0, 128, 128, 0, 0, 0, 0]
 
 
 def tile_st_hmr_pb_kernel(tc, h_new, c_new, g_t, c_g_t, Wg_t, Zg_t_bytes, Zg_t_scale, bg_t, out_0, out_1):
@@ -53,6 +53,8 @@ def tile_st_hmr_pb_kernel(tc, h_new, c_new, g_t, c_g_t, Wg_t, Zg_t_bytes, Zg_t_s
         psum_acc = ctx.enter_context(tc.psum_pool(name="psum_acc", bufs=2))
         ctx.enter_context(tc.manual_schedule())
 
+        zs = const.tile([P, 4], F32, name="zs")
+        nc.scalar.dma_start(out=zs[:], in_=Zg_t_scale.rearrange("a b (p j) c -> p (a b j c)", j=4))
         warm_in = const.tile([P, 1], F32, name="warm_in")
         warm_out = const.tile([P, 1], F32, name="warm_out")
         nc.vector.memset(warm_in[:], 0.0)
@@ -75,8 +77,6 @@ def tile_st_hmr_pb_kernel(tc, h_new, c_new, g_t, c_g_t, Wg_t, Zg_t_bytes, Zg_t_s
             in_=ident_b[:].rearrange("p (r t n) -> p t r n", r=4, t=4),
         )
 
-        zs = const.tile([P, 4], F32, name="zs")
-        nc.sync.dma_start(out=zs[:], in_=Zg_t_scale.rearrange("a b (p j) c -> p (a b j c)", j=4))
 
         wraw = {}
         zraw = {}
@@ -187,11 +187,11 @@ def tile_st_hmr_pb_kernel(tc, h_new, c_new, g_t, c_g_t, Wg_t, Zg_t_bytes, Zg_t_s
             return ap.rearrange("p j (c i) -> p c j i", i=4)
 
         def pool_copy(out, in_):
-            nc.gpsimd.tensor_scalar(out=out, in0=in_, scalar1=1.0, scalar2=0.0, op0=ALU.mult, op1=ALU.add)
+            nc.gpsimd.tensor_scalar(out=near_out(out), in0=near_in(in_), scalar1=1.0, scalar2=0.0, op0=ALU.mult, op1=ALU.add)
 
         def interleave_pool(u):
             grouped[u] = gpool.tile([P, 2, H, 4], BF16, name="grouped", tag="grouped", align_bytes=64)
-            pool_copy(grouped[u][:, 0, ROUTED:H, :], wraw[u][:, :, ROUTED:H].rearrange("p j n -> p n j"))
+            pool_copy(grouped[u][:, 0, ROUTED:H, :], wraw[u][:, :, ROUTED:H])
 
         def alloc_grouped(u):
             if not GP[u]:
@@ -214,7 +214,7 @@ def tile_st_hmr_pb_kernel(tc, h_new, c_new, g_t, c_g_t, Wg_t, Zg_t_bytes, Zg_t_s
             nc.vector.tensor_copy(out=near_out(grouped[u][:, 1, 0 : H - GZ[u], :]), in_=near_in(zwide[u][:, :, 0 : H - GZ[u]]))
 
         def interleave_z_pool(u):
-            pool_copy(grouped[u][:, 1, H - GZ[u] : H, :], zwide[u][:, :, H - GZ[u] : H].rearrange("p j n -> p n j"))
+            pool_copy(grouped[u][:, 1, H - GZ[u] : H, :], zwide[u][:, :, H - GZ[u] : H])
 
         def quantize(u):
             codes[u] = qpool.tile([P, 2 * H], U32, name="codes", tag="codes", align_bytes=64)
@@ -463,8 +463,9 @@ def tile_st_hmr_pb_kernel(tc, h_new, c_new, g_t, c_g_t, Wg_t, Zg_t_bytes, Zg_t_s
         quantize(last - 1)
         multiply(last - 1)
         halves[1] = gpool.tile([P, 2, 2, P, 4], BF16, name="half_b", tag="grouped", align_bytes=64)
-        pool_copy(halves[1][:, :, 0, :, :], wraw[last][:, :, 2 * P : 4 * P].rearrange("p j (f n) -> p f n j", f=2))
-        pool_copy(chunk_tile(3)[:, 1, :, :], zwide[last][:, :, 3 * P : 4 * P].rearrange("p j n -> p n j"))
+        pool_copy(chunk_tile(2)[:, 0, :, :], wraw[last][:, :, 2 * P : 3 * P])
+        pool_copy(chunk_tile(3)[:, 0, :, :], wraw[last][:, :, 3 * P : 4 * P])
+        pool_copy(chunk_tile(3)[:, 1, :, :], zwide[last][:, :, 3 * P : 4 * P])
         for rt in range(2):
             nc.vector.scalar_tensor_tensor(
                 out=tmp[:, rt, :], in0=g_acc[rt][:], scalar=0.25, in1=cg_sb[:, rt, :], op0=ALU.mult, op1=ALU.mult

@@ -21,7 +21,8 @@ ROWS = 256
 NFT = 4
 ROUTED = 256
 RT = [256, 256, 256, 256, 256, 256, 256, 128, 0, 256, 256, 0]
-SH = [0, 0, 0, 0, 0, 0, 0, 0, 96, 0, 0, 0]
+GW = [0, 0, 0, 0, 64, 0, 0, 0, 0, 0, 0, 0]
+SH = [0, 0, 0, 0, 0, 0, 0, 0, 32, 0, 0, 0]
 NV = [3,0,1,0,1,1,1,1,0,1,0,0]
 GP = [0, 0, 0, 0, 0, 0, 0, 1, 1, 0, 0, 0]
 GZ = [0, 0, 0, 0, 0, 0, 128, 128, 0, 0, 0, 0]
@@ -206,7 +207,7 @@ def tile_st_hmr_pb_kernel(tc, h_new, c_new, g_t, c_g_t, Wg_t, Zg_t_bytes, Zg_t_s
 
         def interleave_w(u):
             lo = RT[u] + SH[u]
-            hi = ROUTED if GP[u] else H
+            hi = ROUTED if GP[u] else H - GW[u]
             if lo < hi:
                 nc.vector.tensor_copy(out=near_out(grouped[u][:, 0, lo:hi, :]), in_=near_in(wraw[u][:, :, lo:hi]))
 
@@ -414,6 +415,7 @@ def tile_st_hmr_pb_kernel(tc, h_new, c_new, g_t, c_g_t, Wg_t, Zg_t_bytes, Zg_t_s
                         sum_group(f_acc[rt][:, ft * P : (ft + 1) * P], 0, ft, rt)
             if s == 4:
                 alloc_grouped(4)
+                pool_copy(grouped[4][:, 0, H - GW[4] : H, :], wraw[4][:, :, H - GW[4] : H])
                 interleave_scalar(4)
                 sigmoid(0)
             if c >= 1:

from contextlib import ExitStack

import concourse.masks as masks
import concourse.mybir as mybir

FLOPS = 2 * 2 * 12 * 256 * 512 * 512

F32 = mybir.dt.float32
BF16 = mybir.dt.bfloat16
U32 = mybir.dt.uint32
U8 = mybir.dt.uint8
FP8 = mybir.dt.float8_e4m3fn
FP8X4 = mybir.dt.float8_e4m3fn_x4
ACT = mybir.ActivationFunctionType
ALU = mybir.AluOpType

P = 128
H = 512
T = 4
ROWS = 256
NFT = 4
ROUTED = 256
RT = [256, 256, 256, 256, 256, 256, 256, 128, 0, 256, 256, 0]
GW = [0, 0, 0, 0, 64, 0, 0, 0, 0, 0, 0, 0]
SH = [0, 0, 0, 0, 0, 0, 0, 0, 32, 0, 0, 0]
NV = [3,0,1,0,1,1,1,1,0,1,0,0]
GP = [0, 0, 0, 0, 0, 0, 0, 1, 1, 0, 0, 0]
GZ = [0, 0, 0, 0, 0, 0, 128, 128, 0, 0, 0, 0]


def tile_st_hmr_pb_kernel(tc, h_new, c_new, g_t, c_g_t, Wg_t, Zg_t_bytes, Zg_t_scale, bg_t, out_0, out_1):
    nc = tc.nc
    units = [(g, t) for g in range(3) for t in range(T)]
    n_units = len(units)
    last = n_units - 1

    h_rows = h_new.rearrange("r t n h -> (r t n) h").rearrange("(i p) h -> p i h", p=P)
    c_rows = c_new.rearrange("r t n h -> (r t n) h").rearrange("(i p) h -> p i h", p=P)
    g_rows = g_t.rearrange("r n h -> (r n) h").rearrange("(i p) h -> p i h", p=P)
    cg_rows = c_g_t.rearrange("r n h -> (r n) h").rearrange("(i p) h -> p i h", p=P)
    out0_rows = out_0.rearrange("r n h -> (r n) h").rearrange("(i p) h -> p i h", p=P)
    out1_rows = out_1.rearrange("r n h -> (r n) h").rearrange("(i p) h -> p i h", p=P)

    with ExitStack() as ctx:
        const = ctx.enter_context(tc.tile_pool(name="const", bufs=1))
        wpool = ctx.enter_context(tc.tile_pool(name="wpool", bufs=8))
        zpool = ctx.enter_context(tc.tile_pool(name="zpool", bufs=8))
        zwpool = ctx.enter_context(tc.tile_pool(name="zwpool", bufs=3))
        gpool = ctx.enter_context(tc.tile_pool(name="gpool", bufs=2))
        qpool = ctx.enter_context(tc.tile_pool(name="qpool", bufs=4))
        spool = ctx.enter_context(tc.tile_pool(name="spool", bufs=2))
        psum_mm = ctx.enter_context(tc.psum_pool(name="psum_mm", bufs=4))
        psum_tr = ctx.enter_context(tc.psum_pool(name="psum_tr", bufs=2))
        psum_acc = ctx.enter_context(tc.psum_pool(name="psum_acc", bufs=2))
        ctx.enter_context(tc.manual_schedule())

        zs = const.tile([P, 4], F32, name="zs")
        nc.scalar.dma_start(out=zs[:], in_=Zg_t_scale.rearrange("a b (p j) c -> p (a b j c)", j=4))
        warm_in = const.tile([P, 1], F32, name="warm_in")
        warm_out = const.tile([P, 1], F32, name="warm_out")
        nc.vector.memset(warm_in[:], 0.0)
        nc.scalar.activation(out=warm_out[:], in_=warm_in[:], func=ACT.Sigmoid)
        bias_raw = const.tile([P, P], BF16, name="bias_raw")
        nc.vector.memset(bias_raw[:], 0.0)

        ident_f = const.tile([P, P], F32, name="ident_f")
        masks.make_identity(nc, ident_f[:])
        ident_b = const.tile([P, P], BF16, name="ident_b")
        masks.make_identity(nc, ident_b[:])
        perm_f = const.tile([P, P], F32, name="perm_f")
        nc.vector.tensor_copy(
            out=perm_f[:].rearrange("p (t r n) -> p t r n", t=4, r=4),
            in_=ident_f[:].rearrange("p (r t n) -> p t r n", r=4, t=4),
        )
        perm_b = const.tile([P, P], BF16, name="perm_b")
        nc.vector.tensor_copy(
            out=perm_b[:].rearrange("p (t r n) -> p t r n", t=4, r=4),
            in_=ident_b[:].rearrange("p (r t n) -> p t r n", r=4, t=4),
        )


        wraw = {}
        zraw = {}

        def load_z(u):
            g, t = units[u]
            zraw[u] = zpool.tile([P, 4, H], U8, name="zraw", tag="zraw")
            nc.sync.dma_start(out=zraw[u][:], in_=Zg_t_bytes[g, t].rearrange("(p j) n -> p j n", j=4))

        def load_w(u):
            g, t = units[u]
            wraw[u] = wpool.tile([P, 4, H], BF16, name="wraw", tag="wraw")
            nc.sync.dma_start(out=wraw[u][:], in_=Wg_t[g, t].rearrange("(p j) n -> p j n", j=4))

        h_sb = [const.tile([P, 2, H], BF16, name="h_sb%d" % q) for q in range(4)]
        g_sb = const.tile([P, 2, H], BF16, name="g_sb")
        c_sb = const.tile([P, 8, H], BF16, name="c_sb")
        cg_sb = const.tile([P, 2, H], BF16, name="cg_sb")

        def load_h(q):
            nc.sync.dma_start(out=h_sb[q][:], in_=h_rows[:, 2 * q : 2 * q + 2, :])

        load_z(0)
        load_z(1)
        load_w(0)
        load_w(1)
        load_z(2)
        load_h(0)
        load_h(1)
        load_w(2)
        load_z(3)
        load_h(2)
        load_h(3)
        load_w(3)
        nc.sync.dma_start(out=g_sb[:], in_=g_rows)
        nc.sync.dma_start(out=bias_raw[0:48, :], in_=bg_t.rearrange("g t o (c f) -> (g t o c) f", f=P))
        load_z(4)
        load_w(4)
        nc.sync.dma_start(out=c_sb[:, 0:4, :], in_=c_rows[:, 0:4, :])
        nc.sync.dma_start(out=c_sb[:, 4:8, :], in_=c_rows[:, 4:8, :])
        load_z(5)
        load_w(5)
        load_z(6)
        load_w(6)
        nc.sync.dma_start(out=cg_sb[:], in_=cg_rows)
        load_z(7)
        load_w(7)
        load_z(8)
        load_w(8)
        load_z(9)
        load_w(9)
        load_z(10)
        load_w(10)
        load_z(11)
        load_w(11)

        hg = const.tile([P, T, ROWS, 4], BF16, name="hg", align_bytes=64)
        hg32 = hg[:].rearrange("p t r e -> p (t r e)").bitcast(F32).rearrange("p (t r u) -> p t r u", t=T, u=2)
        gg = const.tile([P, ROWS, 4], BF16, name="gg", align_bytes=64)
        gg32 = gg[:].rearrange("p r e -> p (r e)").bitcast(F32).rearrange("p (i r u) -> p i r u", i=2, u=2)
        bias_sb = const.tile([P, 48], F32, name="bias_sb")
        h_codes = const.tile([P, T * ROWS], U32, name="h_codes", align_bytes=64)
        h_scales = const.tile([P, T * ROWS], U8, name="h_scales", align_bytes=64)
        g_codes = const.tile([P, ROWS], U32, name="g_codes", align_bytes=64)
        g_scales = const.tile([P, ROWS], U8, name="g_scales", align_bytes=64)
        tmp = const.tile([P, 2, H], F32, name="tmp")
        cout = const.tile([P, 2, H], F32, name="cout")
        th = const.tile([P, 2, H], F32, name="th")
        gout = const.tile([P, 2, H], F32, name="gout")

        zwide = {}
        routed = {}
        grouped = {}
        codes = {}
        scales = {}
        banks = {}
        sig = {}

        def widen(u, planes_on_vector):
            zwide[u] = zwpool.tile([P, 4, H], BF16, name="zwide", tag="zwide")
            for j in range(4):
                src = zraw[u][:, j, :].bitcast(FP8)
                if j >= 4 - planes_on_vector:
                    nc.vector.tensor_scalar(
                        out=zwide[u][:, j, :], in0=src, scalar1=zs[:, j : j + 1], scalar2=None, op0=ALU.mult
                    )
                else:
                    nc.scalar.activation(out=zwide[u][:, j, :], in_=src, func=ACT.Copy, scale=zs[:, j : j + 1])

        def route(u):
            if u < 9:
                routed[u] = psum_acc.tile([P, 4 * RT[u]], BF16, name="routed", tag="acc")
            else:
                routed[u] = psum_tr.tile([P, 4 * RT[u]], BF16, name="routed_t", tag="tr")
            for half in range(2):
                nc.tensor.matmul(
                    out=routed[u][:].rearrange("p (n k e) -> p k n e", k=2, e=2)[:, half, :, :],
                    lhsT=ident_b[:],
                    rhs=wraw[u][:, 2 * half : 2 * half + 2, 0 : RT[u]].rearrange("p e n -> p n e"),
                    start=True,
                    stop=True,
                )

        def near_out(ap):
            return ap.rearrange("p (c i) j -> p c j i", i=4)

        def near_in(ap):
            return ap.rearrange("p j (c i) -> p c j i", i=4)

        def pool_copy(out, in_):
            nc.gpsimd.tensor_scalar(out=near_out(out), in0=near_in(in_), scalar1=1.0, scalar2=0.0, op0=ALU.mult, op1=ALU.add)

        def interleave_pool(u):
            grouped[u] = gpool.tile([P, 2, H, 4], BF16, name="grouped", tag="grouped", align_bytes=64)
            pool_copy(grouped[u][:, 0, ROUTED:H, :], wraw[u][:, :, ROUTED:H])

        def alloc_grouped(u):
            if not GP[u]:
                grouped[u] = gpool.tile([P, 2, H, 4], BF16, name="grouped", tag="grouped", align_bytes=64)

        def interleave_scalar(u):
            lo = RT[u]
            if RT[u]:
                nc.scalar.copy(out=grouped[u][:, 0, 0 : RT[u], :].rearrange("p n j -> p (n j)"), in_=routed[u][:])
            if SH[u]:
                nc.scalar.copy(out=near_out(grouped[u][:, 0, lo : lo + SH[u], :]), in_=near_in(wraw[u][:, :, lo : lo + SH[u]]))

        def interleave_w(u):
            lo = RT[u] + SH[u]
            hi = ROUTED if GP[u] else H - GW[u]
            if lo < hi:
                nc.vector.tensor_copy(out=near_out(grouped[u][:, 0, lo:hi, :]), in_=near_in(wraw[u][:, :, lo:hi]))

        def interleave_z(u):
            nc.vector.tensor_copy(out=near_out(grouped[u][:, 1, 0 : H - GZ[u], :]), in_=near_in(zwide[u][:, :, 0 : H - GZ[u]]))

        def interleave_z_pool(u):
            pool_copy(grouped[u][:, 1, H - GZ[u] : H, :], zwide[u][:, :, H - GZ[u] : H])

        def quantize(u):
            codes[u] = qpool.tile([P, 2 * H], U32, name="codes", tag="codes", align_bytes=64)
            scales[u] = qpool.tile([P, 2 * H], U8, name="scales", tag="scales", align_bytes=64)
            nc.vector.quantize_mx(
                out=codes[u][:].bitcast(FP8X4),
                scales=scales[u][:],
                in_=grouped[u][:].rearrange("p a n j -> p (a n j)"),
            )

        def gate_pair(out, u, w_cols, z_cols):
            t = units[u][1]
            nc.tensor.matmul_mx(
                out=out,
                lhsT=codes[u][:, w_cols].bitcast(FP8X4),
                lhsT_scale=scales[u][:, w_cols],
                rhs=h_codes[:, t * ROWS : (t + 1) * ROWS].bitcast(FP8X4),
                rhs_scale=h_scales[:, t * ROWS : (t + 1) * ROWS],
                start=True,
                stop=False,
            )
            nc.tensor.matmul_mx(
                out=out,
                lhsT=codes[u][:, z_cols].bitcast(FP8X4),
                lhsT_scale=scales[u][:, z_cols],
                rhs=g_codes[:].bitcast(FP8X4),
                rhs_scale=g_scales[:],
                start=False,
                stop=True,
            )

        def multiply_part(u, fts):
            for ft in fts:
                if ft == 0:
                    banks[u] = []
                if ft % 2 == 0:
                    banks[u].append(psum_mm.tile([P, 2, ROWS], F32, name="mm", tag="mm"))
                gate_pair(banks[u][ft // 2][:, ft % 2, :], u, slice(ft * P, (ft + 1) * P), slice(H + ft * P, H + (ft + 1) * P))

        def multiply(u):
            multiply_part(u, range(NFT))

        def sigmoid_one(u, ft, src):
            g, t = units[u]
            col = (g * T + t) * NFT + ft
            nc.scalar.activation(out=sig[g][:, ft, t, :], in_=src, func=ACT.Sigmoid, bias=bias_sb[:, col : col + 1])

        def sigmoid(u):
            g, t = units[u]
            if t == 0:
                sig[g] = spool.tile([P, NFT, T, ROWS], F32, name="sig", tag="sig")
            for ft in range(NFT):
                sigmoid_one(u, ft, banks[u][ft // 2][:, ft % 2, :])

        def sum_group(out, g, ft, rt):
            for t in range(T):
                nc.tensor.matmul(
                    out=out,
                    lhsT=sig[g][:, ft, t, rt * P : (rt + 1) * P],
                    rhs=ident_f[:],
                    is_transpose=True,
                    start=(t == 0),
                    stop=(t == T - 1),
                )

        def sum_frames(g, pool, tag):
            accs = []
            for rt in range(2):
                acc = pool.tile([P, H], F32, name="acc_" + tag, tag=tag)
                for ft in range(NFT):
                    sum_group(acc[:, ft * P : (ft + 1) * P], g, ft, rt)
                accs.append(acc)
            return accs

        cts = {}

        def turn_c(ft):
            cts[ft] = psum_tr.tile([P, 8, P], BF16, name="cT", tag="tr")
            for i in range(8):
                nc.tensor.transpose(out=cts[ft][:, i, :], in_=c_sb[:, i, ft * P : (ft + 1) * P], identity=perm_b[:])

        def times_c(ft):
            view = sig[0][:, ft, :, :].rearrange("p t (i r) -> p t i r", i=8)
            nc.vector.tensor_tensor(out=view, in0=view, in1=cts[ft][:].rearrange("p i (t r) -> p t i r", t=T), op=ALU.mult)

        xts = {}

        def turn_h(q):
            xts[q] = psum_mm.tile([P, 2, 2, P], F32, name="xt", tag="mm")
            for i2 in range(2):
                words = h_sb[q][:, i2, :].bitcast(F32)
                for u2 in range(2):
                    nc.tensor.transpose(out=xts[q][:, i2, u2, :], in_=words[:, u2::2], identity=perm_f[:])

        def h_out(q, engine_copy):
            for i2 in range(2):
                i = 2 * q + i2
                engine_copy(
                    out=hg32[:, :, 32 * i : 32 * i + 32, :],
                    in_=xts[q][:, i2, :, :].rearrange("p u (t r) -> p t r u", t=T),
                )

        f_acc = None
        g_acc = None
        o_acc = {}

        def o_sum(u, fts):
            t = units[u][1]
            for ft in fts:
                if t == 0:
                    if ft < 2:
                        o_acc[ft] = psum_tr.tile([P, 2, P], F32, name="o_acc_a", tag="tr")
                    else:
                        o_acc[ft] = psum_acc.tile([P, 2, P], F32, name="o_acc_b", tag="acc")
                for rt in range(2):
                    nc.tensor.matmul(
                        out=o_acc[ft][:, rt, :],
                        lhsT=sig[2][:, ft, t, rt * P : (rt + 1) * P],
                        rhs=ident_f[:],
                        is_transpose=True,
                        start=(t == 0 and rt == 0),
                        stop=(t == T - 1 and rt == 1),
                    )

        EARLY = [4, 10]
        for s in range(n_units):
            a = s - 1
            b = s - 2
            c = s - 3
            if RT[s]:
                route(s)
            if s == 11:
                g_acc = sum_frames(1, psum_tr, "tr")
            if a >= 0 and a not in EARLY:
                alloc_grouped(a)
                if a > 1:
                    interleave_scalar(a)
            if a == 0:
                interleave_z(a)
            if a >= 0:
                interleave_w(a)
            if s == 1 or s == 2:
                turn_h(2 * s - 2)
                turn_h(2 * s - 1)
            if b >= 0:
                quantize(b)
            if s == 4:
                nc.vector.tensor_copy(out=gg32, in_=xg[:].rearrange("p i u r -> p i r u"))
                nc.vector.quantize_mx(
                    out=h_codes[:].bitcast(FP8X4), scales=h_scales[:], in_=hg[:].rearrange("p t r e -> p (t r e)")
                )
                nc.vector.quantize_mx(
                    out=g_codes[:].bitcast(FP8X4), scales=g_scales[:], in_=gg[:].rearrange("p r e -> p (r e)")
                )
            if a >= 1:
                interleave_z(a)
            if s == 3:
                xg = psum_mm.tile([P, 2, 2, P], F32, name="xg", tag="mm")
                for i2 in range(2):
                    words = g_sb[:, i2, :].bitcast(F32)
                    for u2 in range(2):
                        nc.tensor.transpose(out=xg[:, i2, u2, :], in_=words[:, u2::2], identity=ident_f[:])
                bT = psum_tr.tile([P, P], BF16, name="bT", tag="tr")
                nc.tensor.transpose(out=bT[:], in_=bias_raw[:], identity=ident_b[:])
            if GP[s]:
                interleave_pool(s)
                interleave_z_pool(a)
            if s == 7:
                times_c(0)
                times_c(1)
            if s == 8:
                times_c(2)
                times_c(3)
            widen(s, NV[s])
            if s == 1 or s == 2:
                interleave_scalar(a)
            if s == 2 or s == 3:
                h_out(2 * s - 4, nc.scalar.copy)
                h_out(2 * s - 3, nc.scalar.copy)
            if s == 4:
                nc.scalar.copy(out=bias_sb[:], in_=bT[:, 0:48])
                multiply(0)
                multiply(1)
            if b >= 2:
                multiply(b)
            if s == 5:
                turn_c(0)
                turn_c(1)
            if s == 7:
                turn_c(2)
                turn_c(3)
            if s == 8:
                f_acc = [psum_acc.tile([P, H], F32, name="acc_acc", tag="acc") for rt in range(2)]
            if s == 8 or s == 9:
                for rt in range(2):
                    for ft in (2 * (s - 8), 2 * (s - 8) + 1):
                        sum_group(f_acc[rt][:, ft * P : (ft + 1) * P], 0, ft, rt)
            if s == 4:
                alloc_grouped(4)
                pool_copy(grouped[4][:, 0, H - GW[4] : H, :], wraw[4][:, :, H - GW[4] : H])
                interleave_scalar(4)
                sigmoid(0)
            if c >= 1:
                sigmoid(c)
            if s == 10:
                alloc_grouped(10)
                interleave_scalar(10)

        codes[last] = qpool.tile([P, 2 * H], U32, name="codes_l", tag="codes", align_bytes=64)
        scales[last] = qpool.tile([P, 2 * H], U8, name="scales_l", tag="scales", align_bytes=64)

        halves = {}

        def chunk_tile(ft):
            return halves[ft // 2][:, ft % 2, :, :, :]

        def chunk_w(ft):
            nc.vector.tensor_copy(out=near_out(chunk_tile(ft)[:, 0, :, :]), in_=near_in(wraw[last][:, :, ft * P : (ft + 1) * P]))

        def chunk_z(ft, engine_copy):
            engine_copy(out=near_out(chunk_tile(ft)[:, 1, :, :]), in_=near_in(zwide[last][:, :, ft * P : (ft + 1) * P]))

        def chunk_q(ft):
            nc.vector.quantize_mx(
                out=codes[last][:, ft * 2 * P : (ft + 1) * 2 * P].bitcast(FP8X4),
                scales=scales[last][:, ft * 2 * P : (ft + 1) * 2 * P],
                in_=chunk_tile(ft).rearrange("p a n j -> p (a n j)"),
            )

        chunk_mm = {}

        def chunk_multiply(ft):
            chunk_mm[ft] = psum_mm.tile([P, 2, ROWS], F32, name="mm_l", tag="mm")
            base = ft * 2 * P
            gate_pair(chunk_mm[ft][:, 0, :], last, slice(base, base + P), slice(base + P, base + 2 * P))

        def chunk_out(ft):
            cols = slice(ft * P, (ft + 1) * P)
            nc.vector.scalar_tensor_tensor(
                out=gout[:, :, cols], in0=o_acc[ft][:], scalar=0.25, in1=th[:, :, cols], op0=ALU.mult, op1=ALU.mult
            )
            nc.sync.dma_start(out=out0_rows[:, :, cols], in_=gout[:, :, cols])

        all_ft = range(NFT)
        halves[0] = gpool.tile([P, 2, 2, P, 4], BF16, name="half_a", tag="grouped", align_bytes=64)
        chunk_w(0)
        quantize(last - 1)
        multiply(last - 1)
        halves[1] = gpool.tile([P, 2, 2, P, 4], BF16, name="half_b", tag="grouped", align_bytes=64)
        pool_copy(chunk_tile(2)[:, 0, :, :], wraw[last][:, :, 2 * P : 3 * P])
        pool_copy(chunk_tile(3)[:, 0, :, :], wraw[last][:, :, 3 * P : 4 * P])
        pool_copy(chunk_tile(3)[:, 1, :, :], zwide[last][:, :, 3 * P : 4 * P])
        for rt in range(2):
            nc.vector.scalar_tensor_tensor(
                out=tmp[:, rt, :], in0=g_acc[rt][:], scalar=0.25, in1=cg_sb[:, rt, :], op0=ALU.mult, op1=ALU.mult
            )
        for rt in range(2):
            nc.vector.scalar_tensor_tensor(
                out=cout[:, rt, :], in0=f_acc[rt][:], scalar=0.25, in1=tmp[:, rt, :], op0=ALU.mult, op1=ALU.add
            )
            nc.sync.dma_start(out=out1_rows[:, rt, :], in_=cout[:, rt, :])
        o_sum(last - 3, all_ft)
        chunk_z(2, nc.scalar.copy)
        sigmoid(last - 2)
        o_sum(last - 2, all_ft)
        sigmoid(last - 1)
        for rt in range(2):
            nc.scalar.activation(out=th[:, rt, :], in_=cout[:, rt, :], func=ACT.Tanh)
        o_sum(last - 1, (0, 1,))
        chunk_z(0, nc.vector.tensor_copy)
        chunk_w(1)
        chunk_z(1, nc.vector.tensor_copy)
        chunk_q(0)
        chunk_q(1)
        chunk_q(2)
        chunk_q(3)
        for ft in all_ft:
            chunk_multiply(ft)
            sigmoid_one(last, ft, chunk_mm[ft][:, 0, :])
        for ft in all_ft:
            if ft not in (0, 1,):
                o_sum(last - 1, [ft])
            o_sum(last, [ft])
            chunk_out(ft)
